import numpy as np
import ml_dtypes


def mxq(x, axis, fmt="e4m3"):
    dtype, down = {"e4m3": (ml_dtypes.float8_e4m3fn, 7), "e5m2": (ml_dtypes.float8_e5m2, 14)}[fmt]
    v = np.moveaxis(np.asarray(x, np.float32).astype(ml_dtypes.bfloat16).astype(np.float64), axis, -1)
    blocks = v.reshape(v.shape[:-1] + (-1, 32))
    amax = np.abs(blocks).max(-1, keepdims=True)
    byte = np.maximum(np.where(amax > 0, np.frexp(amax)[1] - 1 + 127, 0) - down, 1)
    scale = np.exp2(byte - 127.0)
    codes = (blocks / scale).astype(np.float32).astype(dtype).astype(np.float64)
    return np.moveaxis((codes * scale).reshape(v.shape), -1, axis)


WIDE = False


def mx_kscale(k):
    if not WIDE:
        return np.ones(k)
    levels = np.array([10, -10, 5, -5, 0])
    a = np.random.permutation(np.resize(levels, k // 512 * 4)).reshape(k // 512, 4)
    idx = np.arange(k)
    return np.exp2(a[idx // 512, idx % 128 // 32])


BF16 = ml_dtypes.bfloat16


def bf(x):
    return np.asarray(x, np.float32).astype(BF16)


def f64(x):
    return np.asarray(x).astype(np.float64)


E2M1 = np.array([0.0, 0.5, 1.0, 1.5, 2.0, 3.0, 4.0, 6.0, -0.0, -0.5, -1.0, -1.5, -2.0, -3.0, -4.0, -6.0])


def pack_weight(w, fmt):
    k, n = w.shape
    w = f64(bf(w)).reshape(k // 32, 32, n)
    amax = np.abs(w).max(1)
    if fmt == "e4m3":
        byte = np.frexp(amax)[1] - 1 + 127 - 7
    else:
        mant, ex = np.frexp(amax / 6.0)
        byte = np.where(mant > 0.5, ex, ex - 1) + 127
    byte = np.clip(np.where(amax > 0, byte, 1), 1, 254)
    scaled = (w * np.exp2(127.0 - byte)[:, None, :]).reshape(k, n).astype(np.float32)
    by_word = np.ascontiguousarray(scaled.reshape(k // 512, 128, 4, n).transpose(0, 1, 3, 2))
    if fmt == "e4m3":
        words = by_word.astype(ml_dtypes.float8_e4m3fn).view(np.uint8)
    else:
        c = by_word.astype(ml_dtypes.float4_e2m1fn).view(np.uint8) & 0xF
        words = c[..., 0::2] | (c[..., 1::2] << 4)
    return np.ascontiguousarray(words), np.ascontiguousarray(byte.astype(np.uint8).reshape(k // 512, 16, n))


def unpack_weight(words, scales, fmt):
    g, p, n, _ = words.shape
    if fmt == "e4m3":
        vals = np.ascontiguousarray(words).view(ml_dtypes.float8_e4m3fn).astype(np.float64)
    else:
        nib = np.empty((g, p, n, 4), np.uint8)
        nib[..., 0::2] = words & 0xF
        nib[..., 1::2] = words >> 4
        vals = E2M1[nib]
    vals = vals * np.repeat(np.exp2(scales.astype(np.float64) - 127.0), 8, axis=1)[..., None]
    return vals.transpose(0, 1, 3, 2).reshape(g * 512, n)

def pack4(w):
    words, scales = pack_weight(w, "e2m1")
    return words.reshape(words.shape[0], 128, -1), scales


def unpack4(words, scales):
    return unpack_weight(words.reshape(words.shape[0], 128, -1, 2), scales, "e2m1")


B, N, SIZE, CH = 512, 32, 512, 256


def sigmoid(v):
    return 1.0 / (1.0 + np.exp(-v))


def setup_inputs():
    s = mx_kscale(SIZE)
    half = np.concatenate([np.ones(CH), np.full(CH, 2.0 / np.sqrt(N))])
    z_node = bf(np.random.standard_normal((B, N, SIZE)) * s)
    z_children = bf(np.random.standard_normal((B, N, SIZE)) * half)
    w_f = np.random.standard_normal((CH, SIZE)) / np.sqrt(SIZE) / s
    words, scales = pack4(np.ascontiguousarray(w_f.T))
    U_f = bf(np.random.standard_normal((CH, CH)) / np.sqrt(CH))
    b_f = bf(np.random.standard_normal(CH) * 0.5)
    return {"z_node": z_node,
            "z_children": z_children,
            "W_f_words": words,
            "W_f_scales": scales,
            "U_f": U_f,
            "b_f": b_f}


def reference(z_node, z_children, W_f_words, W_f_scales, U_f, b_f):
    h_k = f64(z_children)[..., :CH]
    c_k = f64(z_children)[..., CH:]
    f_j_k = sigmoid((mxq(f64(z_node), 2, "e4m3") @ unpack4(W_f_words, W_f_scales)) + h_k @ f64(U_f).T + f64(b_f))
    return (f_j_k * c_k).sum(axis=1)

@@ -1,0 +1,191 @@
+from concourse import mybir
+from concourse.masks import make_identity
+
+F32 = mybir.dt.float32
+BF16 = mybir.dt.bfloat16
+U8 = mybir.dt.uint8
+U32 = mybir.dt.uint32
+I32 = mybir.dt.int32
+FP8X4 = mybir.dt.float8_e4m3fn_x4
+FP4X4 = mybir.dt.float4_e2m1fn_x4
+ADD = mybir.AluOpType.add
+MULT = mybir.AluOpType.mult
+SIGMOID = mybir.ActivationFunctionType.Sigmoid
+
+P = 128
+NODES, CHILDREN, SIZE, CH = 512, 32, 512, 256
+ROUND = 4
+PAIR = 2
+PAIRS = ROUND // PAIR
+ROUNDS_PER_TILE = CHILDREN // ROUND
+ROUNDS = (NODES // P) * ROUNDS_PER_TILE
+WORDS = SIZE // 2
+
+FLOPS = 2 * NODES * CHILDREN * CH * (SIZE + CH)
+
+
+def tile_treelstm_pa_t_kernel(tc, z_node, z_children, W_f_words, W_f_scales, U_f, b_f, out):
+    nc = tc.nc
+    with (
+        tc.tile_pool(name="const", bufs=1) as const,
+        tc.tile_pool(name="loads", bufs=4) as loads,
+        tc.tile_pool(name="work", bufs=4) as work,
+        tc.psum_pool(name="psum", bufs=2) as psum,
+        tc.manual_schedule(),
+    ):
+        z_in, zc_in, zT_ps, hT_ps, z_codes, z_scales, hT_sb = {}, {}, {}, {}, {}, {}, {}
+        grouped, mx_ps, hu_ps, gate, gated, sums = {}, {}, {}, {}, {}, {}
+
+        def load(r):
+            node_tile, j = divmod(r, ROUNDS_PER_TILE)
+            rows = slice(node_tile * P, (node_tile + 1) * P)
+            kids = slice(j * ROUND, (j + 1) * ROUND)
+            zc_in[r] = loads.tile([P, ROUND, SIZE], BF16, name="zc_in", bufs=6)
+            nc.sync.dma_start(out=zc_in[r][:], in_=z_children[rows, kids, :])
+            z_in[r] = loads.tile([P, ROUND, SIZE], BF16, name="z_in")
+            nc.sync.dma_start(out=z_in[r][:], in_=z_node[rows, kids, :])
+
+        def transpose(r):
+            hT_ps[r] = psum.tile([P, ROUND, P], F32, name="hT_ps")
+            zc_words = zc_in[r][:].bitcast(F32)
+            for i in range(ROUND):
+                nc.tensor.transpose(hT_ps[r][:, i, :], zc_words[:, i, 0 : CH // 2], ident[:])
+            z_words = z_in[r][:].bitcast(F32)
+            zT_ps[r] = []
+            for pair in range(PAIRS):
+                bank = psum.tile([P, PAIR, 2, P], F32, name="zT_ps")
+                for i in range(PAIR):
+                    for u in range(2):
+                        nc.tensor.transpose(bank[:, i, u, :], z_words[:, pair * PAIR + i, u:WORDS:2], ident[:])
+                zT_ps[r].append(bank)
+
+        def leave_psum(r):
+            hT_sb[r] = work.tile([P, ROUND, P], F32, name="hT_sb")
+            nc.scalar.copy(out=hT_sb[r][:], in_=hT_ps[r][:])
+            grouped[r] = []
+            for pair in range(PAIRS):
+                values = work.tile([P, PAIR, P, 4], BF16, name="grouped", align_bytes=64)
+                nc.scalar.copy(out=values[:].bitcast(F32), in_=zT_ps[r][pair][:].rearrange("p i u b -> p i b u"))
+                grouped[r].append(values)
+
+        def quantise(r):
+            z_codes[r] = []
+            z_scales[r] = []
+            for pair in range(PAIRS):
+                codes = work.tile([P, PAIR * P], U32, align_bytes=64)
+                scales = work.tile([P, PAIR * P], U8, align_bytes=64)
+                nc.vector.quantize_mx(
+                    out=codes[:].bitcast(FP8X4),
+                    scales=scales[:],
+                    in_=grouped[r][pair][:].rearrange("p i b t -> p (i b t)"),
+                )
+                z_codes[r].append(codes)
+                z_scales[r].append(scales)
+
+        def multiply(r):
+            hT = hT_sb[r][:].bitcast(BF16).rearrange("p i (b e) -> p i b e", e=2)
+            hu_ps[r] = []
+            for pair in range(PAIRS):
+                bank = psum.tile([P, PAIR, CH], F32, name="hu_ps")
+                for i in range(PAIR):
+                    for e in range(2):
+                        nc.tensor.matmul(
+                            bank[:, i, :],
+                            lhsT=hT[:, pair * PAIR + i, :, e],
+                            rhs=uT[:, :, e],
+                            start=(e == 0),
+                            stop=(e == 1),
+                        )
+                hu_ps[r].append(bank)
+            mx_ps[r] = []
+            for pair in range(PAIRS):
+                bank = psum.tile([P, PAIR, CH], F32, name="mx_ps")
+                for i in range(PAIR):
+                    nc.tensor.matmul_mx(
+                        out=bank[:, i, :],
+                        lhsT=z_codes[r][pair][:, i * P : (i + 1) * P].bitcast(FP8X4),
+                        lhsT_scale=z_scales[r][pair][:, i * P : (i + 1) * P],
+                        rhs=w_codes[:].bitcast(FP4X4),
+                        rhs_scale=w_scales[:],
+                        start=True,
+                        stop=True,
+                    )
+                mx_ps[r].append(bank)
+
+        def add_terms(r):
+            gate[r] = work.tile([P, ROUND, CH], F32, name="gate")
+            for pair in range(PAIRS):
+                half = gate[r][:, pair * PAIR : (pair + 1) * PAIR, :]
+                nc.vector.tensor_tensor(out=half, in0=hu_ps[r][pair][:], in1=bias, op=ADD)
+            for pair in range(PAIRS):
+                half = gate[r][:, pair * PAIR : (pair + 1) * PAIR, :]
+                nc.vector.tensor_tensor(out=half, in0=mx_ps[r][pair][:], in1=half, op=ADD)
+
+        def squash_and_weigh(r):
+            node_tile, j = divmod(r, ROUNDS_PER_TILE)
+            nc.scalar.activation(out=gate[r][:], in_=gate[r][:], func=SIGMOID)
+            if j == 0:
+                sums[node_tile] = work.tile([P, 2, ROUND, CH], F32, name="sums", bufs=2)
+            if j < 2:
+                gated[r] = sums[node_tile][:, j, :, :]
+            else:
+                gated_sb = work.tile([P, ROUND, CH], F32)
+                gated[r] = gated_sb[:]
+            nc.gpsimd.tensor_tensor(out=gated[r], in0=gate[r][:], in1=zc_in[r][:, :, CH:SIZE], op=MULT)
+
+        def accumulate(r):
+            node_tile, j = divmod(r, ROUNDS_PER_TILE)
+            if j >= 2:
+                adder = nc.gpsimd if j % 2 == 0 else nc.vector
+                running = sums[node_tile][:, j % 2, :, :]
+                adder.tensor_tensor(out=running, in0=running, in1=gated[r], op=ADD)
+            if j == ROUNDS_PER_TILE - 1:
+                out_sb = work.tile([P, CH], F32, bufs=2)
+                nc.vector.tensor_reduce(
+                    out=out_sb[:],
+                    in_=sums[node_tile][:].rearrange("p g i c -> p c (g i)"),
+                    axis=mybir.AxisListType.X,
+                    op=ADD,
+                )
+                nc.sync.dma_start(out=out[node_tile * P : (node_tile + 1) * P, :], in_=out_sb[:])
+
+        def run(stage, r):
+            if 0 <= r < ROUNDS:
+                stage(r)
+
+        ident = const.tile([P, P], F32)
+        make_identity(nc, ident[:])
+        w_scales = const.tile([P, CH], U8, align_bytes=64)
+        nc.vector.memset(w_scales[:].bitcast(I32), 0)
+
+        u_rows = const.tile([P, 2, CH], BF16)
+        nc.sync.dma_start(out=u_rows[:], in_=U_f.rearrange("(a p) k -> p a k", p=P))
+        load(0)
+        w_codes = const.tile([P, 2 * CH], U8, align_bytes=64)
+        nc.sync.dma_start(out=w_codes[:].bitcast(I32), in_=W_f_words[0].bitcast(I32))
+        for quadrant in range(4):
+            nc.sync.dma_start(
+                out=w_scales[32 * quadrant : 32 * quadrant + 4, :].bitcast(I32),
+                in_=W_f_scales[0, 4 * quadrant : 4 * quadrant + 4, :].bitcast(I32),
+            )
+        load(1)
+        b_rows = const.tile([P, CH], BF16)
+        nc.sync.dma_start(out=b_rows[:], in_=b_f.partition_broadcast(P))
+
+        u_ps = psum.tile([P, ROUND, P], F32, name="hT_ps")
+        for a in range(2):
+            nc.tensor.transpose(u_ps[:, a, :], u_rows[:].bitcast(F32)[:, a, :], ident[:])
+        uT_words = const.tile([P, 2, P], F32)
+        nc.vector.tensor_copy(out=uT_words[:], in_=u_ps[:, 0:2, :])
+        uT = uT_words[:].bitcast(BF16).rearrange("p a (c e) -> p (a c) e", e=2)
+        bias = b_rows[:].unsqueeze(1).to_broadcast([P, PAIR, CH])
+
+        for step in range(-2, ROUNDS + 2):
+            run(load, step + 4)
+            run(quantise, step + 1)
+            run(squash_and_weigh, step - 1)
+            run(multiply, step)
+            run(transpose, step + 2)
+            run(leave_psum, step + 2)
+            run(add_terms, step)
+            run(accumulate, step - 2)

@@ -125,25 +125,21 @@ def tile_treelstm_pa_t_kernel(tc, z_node, z_children, W_f_words, W_f_scales, U_f
             node_tile, j = divmod(r, ROUNDS_PER_TILE)
             nc.scalar.activation(out=gate[r][:], in_=gate[r][:], func=SIGMOID)
             if j == 0:
-                sums[node_tile] = work.tile([P, 2, ROUND, CH], F32, name="sums", bufs=2)
-            if j < 2:
-                gated[r] = sums[node_tile][:, j, :, :]
+                sums[node_tile] = work.tile([P, ROUND, CH], F32, name="sums", bufs=2)
+                gated[r] = sums[node_tile]
             else:
-                gated_sb = work.tile([P, ROUND, CH], F32)
-                gated[r] = gated_sb[:]
-            nc.gpsimd.tensor_tensor(out=gated[r], in0=gate[r][:], in1=zc_in[r][:, :, CH:SIZE], op=MULT)
+                gated[r] = work.tile([P, ROUND, CH], F32, name="gated", bufs=1)
+            nc.gpsimd.tensor_tensor(out=gated[r][:], in0=gate[r][:], in1=zc_in[r][:, :, CH:SIZE], op=MULT)
 
         def accumulate(r):
             node_tile, j = divmod(r, ROUNDS_PER_TILE)
-            if j >= 2:
-                adder = nc.gpsimd if j % 2 == 0 else nc.vector
-                running = sums[node_tile][:, j % 2, :, :]
-                adder.tensor_tensor(out=running, in0=running, in1=gated[r], op=ADD)
+            if j > 0:
+                nc.vector.tensor_tensor(out=sums[node_tile][:], in0=sums[node_tile][:], in1=gated[r][:], op=ADD)
             if j == ROUNDS_PER_TILE - 1:
                 out_sb = work.tile([P, CH], F32, bufs=2)
                 nc.vector.tensor_reduce(
                     out=out_sb[:],
-                    in_=sums[node_tile][:].rearrange("p g i c -> p c (g i)"),
+                    in_=sums[node_tile][:].rearrange("p i c -> p c i"),
                     axis=mybir.AxisListType.X,
                     op=ADD,
                 )
@@ -183,9 +179,9 @@ def tile_treelstm_pa_t_kernel(tc, z_node, z_children, W_f_words, W_f_scales, U_f
         for step in range(-2, ROUNDS + 2):
             run(load, step + 4)
             run(quantise, step + 1)
+            run(accumulate, step - 2)
             run(squash_and_weigh, step - 1)
             run(multiply, step)
             run(transpose, step + 2)
             run(leave_psum, step + 2)
             run(add_terms, step)
-            run(accumulate, step - 2)

@@ -34,7 +34,7 @@ def tile_treelstm_pa_t_kernel(tc, z_node, z_children, W_f_words, W_f_scales, U_f
         tc.manual_schedule(),
     ):
         z_in, zc_in, zT_ps, hT_ps, z_codes, z_scales, hT_sb = {}, {}, {}, {}, {}, {}, {}
-        grouped, mx_ps, hu_ps, gate, gated, sums = {}, {}, {}, {}, {}, {}
+        grouped, mx_ps, hu_ps, gate, gated, sumsT_ps, sumsT_sb = {}, {}, {}, {}, {}, {}, {}
 
         def load(r):
             node_tile, j = divmod(r, ROUNDS_PER_TILE)
@@ -46,7 +46,7 @@ def tile_treelstm_pa_t_kernel(tc, z_node, z_children, W_f_words, W_f_scales, U_f
             nc.sync.dma_start(out=z_in[r][:], in_=z_node[rows, kids, :])
 
         def transpose(r):
-            hT_ps[r] = psum.tile([P, ROUND, P], F32, name="hT_ps")
+            hT_ps[r] = psum.tile([P, ROUND, P], F32, name="hT_ps", bufs=1)
             zc_words = zc_in[r][:].bitcast(F32)
             for i in range(ROUND):
                 nc.tensor.transpose(hT_ps[r][:, i, :], zc_words[:, i, 0 : CH // 2], ident[:])
@@ -122,28 +122,39 @@ def tile_treelstm_pa_t_kernel(tc, z_node, z_children, W_f_words, W_f_scales, U_f
                 nc.vector.tensor_tensor(out=half, in0=mx_ps[r][pair][:], in1=half, op=ADD)
 
         def squash_and_weigh(r):
-            node_tile, j = divmod(r, ROUNDS_PER_TILE)
             nc.scalar.activation(out=gate[r][:], in_=gate[r][:], func=SIGMOID)
-            if j == 0:
-                sums[node_tile] = work.tile([P, ROUND, CH], F32, name="sums", bufs=2)
-                gated[r] = sums[node_tile]
-            else:
-                gated[r] = work.tile([P, ROUND, CH], F32, name="gated", bufs=1)
+            gated[r] = work.tile([P, ROUND, CH], F32, name="gated")
             nc.gpsimd.tensor_tensor(out=gated[r][:], in0=gate[r][:], in1=zc_in[r][:, :, CH:SIZE], op=MULT)
 
-        def accumulate(r):
+        def add_up(r):
             node_tile, j = divmod(r, ROUNDS_PER_TILE)
-            if j > 0:
-                nc.vector.tensor_tensor(out=sums[node_tile][:], in0=sums[node_tile][:], in1=gated[r][:], op=ADD)
+            if j == 0:
+                sumsT_ps[node_tile] = psum.tile([P, 2, P], F32, name="sumsT_ps", bufs=1)
+            for i in range(ROUND):
+                for a in range(2):
+                    nc.tensor.matmul(
+                        sumsT_ps[node_tile][:, a, :],
+                        lhsT=gated[r][:, i, a * P : (a + 1) * P],
+                        rhs=ident[:],
+                        is_transpose=True,
+                        start=(j == 0 and i == 0 and a == 0),
+                        stop=(j == ROUNDS_PER_TILE - 1 and i == ROUND - 1 and a == 1),
+                    )
             if j == ROUNDS_PER_TILE - 1:
-                out_sb = work.tile([P, CH], F32, bufs=2)
-                nc.vector.tensor_reduce(
-                    out=out_sb[:],
-                    in_=sums[node_tile][:].rearrange("p i c -> p c i"),
-                    axis=mybir.AxisListType.X,
-                    op=ADD,
+                sumsT_sb[node_tile] = work.tile([P, 2, P], F32, name="sumsT_sb", bufs=2)
+                nc.scalar.copy(out=sumsT_sb[node_tile][:], in_=sumsT_ps[node_tile][:])
+
+        def store(r):
+            node_tile, j = divmod(r, ROUNDS_PER_TILE)
+            if j == ROUNDS_PER_TILE - 1:
+                sums_ps = psum.tile([P, ROUND, P], F32, name="hT_ps", bufs=1)
+                for a in range(2):
+                    nc.tensor.transpose(sums_ps[:, a, :], sumsT_sb[node_tile][:, a, :], ident[:])
+                out_sb = work.tile([P, 2, P], F32, bufs=2)
+                nc.scalar.copy(out=out_sb[:], in_=sums_ps[:, 0:2, :])
+                nc.sync.dma_start(
+                    out=out[node_tile * P : (node_tile + 1) * P, :], in_=out_sb[:].rearrange("p a c -> p (a c)")
                 )
-                nc.sync.dma_start(out=out[node_tile * P : (node_tile + 1) * P, :], in_=out_sb[:])
 
         def run(stage, r):
             if 0 <= r < ROUNDS:
@@ -168,7 +179,7 @@ def tile_treelstm_pa_t_kernel(tc, z_node, z_children, W_f_words, W_f_scales, U_f
         b_rows = const.tile([P, CH], BF16)
         nc.sync.dma_start(out=b_rows[:], in_=b_f.partition_broadcast(P))
 
-        u_ps = psum.tile([P, ROUND, P], F32, name="hT_ps")
+        u_ps = psum.tile([P, ROUND, P], F32, name="hT_ps", bufs=1)
         for a in range(2):
             nc.tensor.transpose(u_ps[:, a, :], u_rows[:].bitcast(F32)[:, a, :], ident[:])
         uT_words = const.tile([P, 2, P], F32)
@@ -176,12 +187,13 @@ def tile_treelstm_pa_t_kernel(tc, z_node, z_children, W_f_words, W_f_scales, U_f
         uT = uT_words[:].bitcast(BF16).rearrange("p a (c e) -> p (a c) e", e=2)
         bias = b_rows[:].unsqueeze(1).to_broadcast([P, PAIR, CH])
 
-        for step in range(-2, ROUNDS + 2):
+        for step in range(-2, ROUNDS + 4):
             run(load, step + 4)
             run(quantise, step + 1)
-            run(accumulate, step - 2)
             run(squash_and_weigh, step - 1)
             run(multiply, step)
+            run(store, step - 3)
+            run(add_up, step - 2)
             run(transpose, step + 2)
             run(leave_psum, step + 2)
             run(add_terms, step)

@@ -82,21 +82,23 @@ def tile_treelstm_pa_t_kernel(tc, z_node, z_children, W_f_words, W_f_scales, U_f
                 z_codes[r].append(codes)
                 z_scales[r].append(scales)
 
-        def multiply(r):
+        def multiply_plain(r, pair):
             hT = hT_sb[r][:].bitcast(BF16).rearrange("p i (b e) -> p i b e", e=2)
+            bank = psum.tile([P, PAIR, CH], F32, name="hu_ps")
+            for i in range(PAIR):
+                for e in range(2):
+                    nc.tensor.matmul(
+                        bank[:, i, :],
+                        lhsT=hT[:, pair * PAIR + i, :, e],
+                        rhs=uT[:, :, e],
+                        start=(e == 0),
+                        stop=(e == 1),
+                    )
+            hu_ps[r].append(bank)
+
+        def multiply(r):
             hu_ps[r] = []
-            for pair in range(PAIRS):
-                bank = psum.tile([P, PAIR, CH], F32, name="hu_ps")
-                for i in range(PAIR):
-                    for e in range(2):
-                        nc.tensor.matmul(
-                            bank[:, i, :],
-                            lhsT=hT[:, pair * PAIR + i, :, e],
-                            rhs=uT[:, :, e],
-                            start=(e == 0),
-                            stop=(e == 1),
-                        )
-                hu_ps[r].append(bank)
+            multiply_plain(r, 0)
             mx_ps[r] = []
             for pair in range(PAIRS):
                 bank = psum.tile([P, PAIR, CH], F32, name="mx_ps")
@@ -111,15 +113,16 @@ def tile_treelstm_pa_t_kernel(tc, z_node, z_children, W_f_words, W_f_scales, U_f
                         stop=True,
                     )
                 mx_ps[r].append(bank)
+            multiply_plain(r, 1)
 
         def add_terms(r):
             gate[r] = work.tile([P, ROUND, CH], F32, name="gate")
-            for pair in range(PAIRS):
-                half = gate[r][:, pair * PAIR : (pair + 1) * PAIR, :]
-                nc.vector.tensor_tensor(out=half, in0=hu_ps[r][pair][:], in1=bias, op=ADD)
-            for pair in range(PAIRS):
-                half = gate[r][:, pair * PAIR : (pair + 1) * PAIR, :]
-                nc.vector.tensor_tensor(out=half, in0=mx_ps[r][pair][:], in1=half, op=ADD)
+            first = gate[r][:, 0:PAIR, :]
+            second = gate[r][:, PAIR:ROUND, :]
+            nc.vector.tensor_tensor(out=first, in0=hu_ps[r][0][:], in1=bias, op=ADD)
+            nc.vector.tensor_tensor(out=second, in0=mx_ps[r][1][:], in1=bias, op=ADD)
+            nc.vector.tensor_tensor(out=first, in0=mx_ps[r][0][:], in1=first, op=ADD)
+            nc.vector.tensor_tensor(out=second, in0=hu_ps[r][1][:], in1=second, op=ADD)
 
         def squash_and_weigh(r):
             nc.scalar.activation(out=gate[r][:], in_=gate[r][:], func=SIGMOID)

@@ -19,6 +19,7 @@ PAIR = 2
 PAIRS = ROUND // PAIR
 ROUNDS_PER_TILE = CHILDREN // ROUND
 ROUNDS = (NODES // P) * ROUNDS_PER_TILE
+FIRST_PAIR, SECOND_PAIR, WHOLE_ROUND = slice(0, PAIR), slice(PAIR, ROUND), slice(0, ROUND)
 WORDS = SIZE // 2
 
 FLOPS = 2 * NODES * CHILDREN * CH * (SIZE + CH)
@@ -34,16 +35,23 @@ def tile_treelstm_pa_t_kernel(tc, z_node, z_children, W_f_words, W_f_scales, U_f
         tc.manual_schedule(),
     ):
         z_in, zc_in, zT_ps, hT_ps, z_codes, z_scales, hT_sb = {}, {}, {}, {}, {}, {}, {}
-        grouped, mx_ps, hu_ps, gate, gated, sumsT_ps, sumsT_sb = {}, {}, {}, {}, {}, {}, {}
+        grouped, mx_ps, hu_ps, gate, gated, sumsT_ps, sumsT_sb, z_sorted = {}, {}, {}, {}, {}, {}, {}, {}
 
         def load(r):
             node_tile, j = divmod(r, ROUNDS_PER_TILE)
             rows = slice(node_tile * P, (node_tile + 1) * P)
             kids = slice(j * ROUND, (j + 1) * ROUND)
-            zc_in[r] = loads.tile([P, ROUND, SIZE], BF16, name="zc_in", bufs=6)
+            zc_in[r] = loads.tile([P, ROUND, SIZE], BF16, name="zc_in", bufs=8)
             nc.sync.dma_start(out=zc_in[r][:], in_=z_children[rows, kids, :])
-            z_in[r] = loads.tile([P, ROUND, SIZE], BF16, name="z_in")
+            z_in[r] = loads.tile([P, ROUND, SIZE], BF16, name="z_in", bufs=6)
             nc.sync.dma_start(out=z_in[r][:], in_=z_node[rows, kids, :])
+
+        def sort_words(r):
+            z_sorted[r] = loads.tile([P, PAIR, 2, P], F32, name="z_sorted", bufs=3)
+            nc.vector.tensor_copy(
+                out=z_sorted[r][:],
+                in_=z_in[r][:, SECOND_PAIR, :].bitcast(F32).rearrange("p i (w u) -> p i u w", u=2),
+            )
 
         def transpose(r):
             hT_ps[r] = psum.tile([P, ROUND, P], F32, name="hT_ps", bufs=1)
@@ -56,7 +64,10 @@ def tile_treelstm_pa_t_kernel(tc, z_node, z_children, W_f_words, W_f_scales, U_f
                 bank = psum.tile([P, PAIR, 2, P], F32, name="zT_ps")
                 for i in range(PAIR):
                     for u in range(2):
-                        nc.tensor.transpose(bank[:, i, u, :], z_words[:, pair * PAIR + i, u:WORDS:2], ident[:])
+                        if pair == 0:
+                            nc.tensor.transpose(bank[:, i, u, :], z_words[:, i, u:WORDS:2], ident[:])
+                        else:
+                            nc.tensor.transpose(bank[:, i, u, :], z_sorted[r][:, i, u, :], ident[:])
                 zT_ps[r].append(bank)
 
         def leave_psum(r):
@@ -124,10 +135,24 @@ def tile_treelstm_pa_t_kernel(tc, z_node, z_children, W_f_words, W_f_scales, U_f
             nc.vector.tensor_tensor(out=first, in0=mx_ps[r][0][:], in1=first, op=ADD)
             nc.vector.tensor_tensor(out=second, in0=hu_ps[r][1][:], in1=second, op=ADD)
 
+        def squash(r, kids):
+            nc.scalar.activation(out=gate[r][:, kids, :], in_=gate[r][:, kids, :], func=SIGMOID)
+
+        def weigh(engine, r, kids):
+            engine.tensor_tensor(out=gated[r][:, kids, :], in0=gate[r][:, kids, :], in1=zc_in[r][:, kids, CH:SIZE], op=MULT)
+
         def squash_and_weigh(r):
-            nc.scalar.activation(out=gate[r][:], in_=gate[r][:], func=SIGMOID)
             gated[r] = work.tile([P, ROUND, CH], F32, name="gated")
-            nc.gpsimd.tensor_tensor(out=gated[r][:], in0=gate[r][:], in1=zc_in[r][:, :, CH:SIZE], op=MULT)
+            if r == ROUNDS - 1:
+                for kids in (FIRST_PAIR, SECOND_PAIR):
+                    squash(r, kids)
+                    weigh(nc.vector, r, kids)
+            elif r == ROUNDS - 2:
+                squash(r, WHOLE_ROUND)
+                weigh(nc.gpsimd, r, FIRST_PAIR)
+            else:
+                squash(r, WHOLE_ROUND)
+                weigh(nc.gpsimd, r, WHOLE_ROUND)
 
         def add_up(r):
             node_tile, j = divmod(r, ROUNDS_PER_TILE)
@@ -181,6 +206,8 @@ def tile_treelstm_pa_t_kernel(tc, z_node, z_children, W_f_words, W_f_scales, U_f
         load(1)
         b_rows = const.tile([P, CH], BF16)
         nc.sync.dma_start(out=b_rows[:], in_=b_f.partition_broadcast(P))
+        load(2)
+        load(3)
 
         u_ps = psum.tile([P, ROUND, P], F32, name="hT_ps", bufs=1)
         for a in range(2):
@@ -190,8 +217,9 @@ def tile_treelstm_pa_t_kernel(tc, z_node, z_children, W_f_words, W_f_scales, U_f
         uT = uT_words[:].bitcast(BF16).rearrange("p a (c e) -> p (a c) e", e=2)
         bias = b_rows[:].unsqueeze(1).to_broadcast([P, PAIR, CH])
 
+        sort_words(0)
         for step in range(-2, ROUNDS + 4):
-            run(load, step + 4)
+            run(load, step + 6)
             run(quantise, step + 1)
             run(squash_and_weigh, step - 1)
             run(multiply, step)
@@ -200,3 +228,6 @@ def tile_treelstm_pa_t_kernel(tc, z_node, z_children, W_f_words, W_f_scales, U_f
             run(transpose, step + 2)
             run(leave_psum, step + 2)
             run(add_terms, step)
+            if step - 1 == ROUNDS - 2:
+                weigh(nc.vector, step - 1, SECOND_PAIR)
+            run(sort_words, step + 3)

@@ -101,7 +101,7 @@ def tile_treelstm_pa_t_kernel(tc, z_node, z_children, W_f_words, W_f_scales, U_f
                     nc.tensor.matmul(
                         bank[:, i, :],
                         lhsT=hT[:, pair * PAIR + i, :, e],
-                        rhs=uT[:, :, e],
+                        rhs=uT[:, e, :],
                         start=(e == 0),
                         stop=(e == 1),
                     )
@@ -188,6 +188,9 @@ def tile_treelstm_pa_t_kernel(tc, z_node, z_children, W_f_words, W_f_scales, U_f
             if 0 <= r < ROUNDS:
                 stage(r)
 
+        warm = const.tile([P, 2], F32)
+        nc.vector.memset(warm[:], 0.0)
+        nc.scalar.activation(out=warm[:, 1:2], in_=warm[:, 0:1], func=SIGMOID)
         ident = const.tile([P, P], F32)
         make_identity(nc, ident[:])
         w_scales = const.tile([P, CH], U8, align_bytes=64)
@@ -214,7 +217,11 @@ def tile_treelstm_pa_t_kernel(tc, z_node, z_children, W_f_words, W_f_scales, U_f
             nc.tensor.transpose(u_ps[:, a, :], u_rows[:].bitcast(F32)[:, a, :], ident[:])
         uT_words = const.tile([P, 2, P], F32)
         nc.vector.tensor_copy(out=uT_words[:], in_=u_ps[:, 0:2, :])
-        uT = uT_words[:].bitcast(BF16).rearrange("p a (c e) -> p (a c) e", e=2)
+        uT = const.tile([P, 2, CH], BF16)
+        nc.vector.tensor_copy(
+            out=uT[:].rearrange("p e (a c) -> p e a c", a=2),
+            in_=uT_words[:].bitcast(BF16).rearrange("p a (c e) -> p e a c", e=2),
+        )
         bias = b_rows[:].unsqueeze(1).to_broadcast([P, PAIR, CH])
 
         sort_words(0)

@@ -35,7 +35,7 @@ def tile_treelstm_pa_t_kernel(tc, z_node, z_children, W_f_words, W_f_scales, U_f
         tc.manual_schedule(),
     ):
         z_in, zc_in, zT_ps, hT_ps, z_codes, z_scales, hT_sb = {}, {}, {}, {}, {}, {}, {}
-        grouped, mx_ps, hu_ps, gate, gated, sumsT_ps, sumsT_sb, z_sorted = {}, {}, {}, {}, {}, {}, {}, {}
+        grouped, mx_ps, hu_ps, gate, gated, sumsT_ps, sumsT_sb = {}, {}, {}, {}, {}, {}, {}
 
         def load(r):
             node_tile, j = divmod(r, ROUNDS_PER_TILE)
@@ -45,13 +45,6 @@ def tile_treelstm_pa_t_kernel(tc, z_node, z_children, W_f_words, W_f_scales, U_f
             nc.sync.dma_start(out=zc_in[r][:], in_=z_children[rows, kids, :])
             z_in[r] = loads.tile([P, ROUND, SIZE], BF16, name="z_in", bufs=6)
             nc.sync.dma_start(out=z_in[r][:], in_=z_node[rows, kids, :])
-
-        def sort_words(r):
-            z_sorted[r] = loads.tile([P, PAIR, 2, P], F32, name="z_sorted", bufs=3)
-            nc.vector.tensor_copy(
-                out=z_sorted[r][:],
-                in_=z_in[r][:, SECOND_PAIR, :].bitcast(F32).rearrange("p i (w u) -> p i u w", u=2),
-            )
 
         def transpose(r):
             hT_ps[r] = psum.tile([P, ROUND, P], F32, name="hT_ps", bufs=1)
@@ -64,15 +57,15 @@ def tile_treelstm_pa_t_kernel(tc, z_node, z_children, W_f_words, W_f_scales, U_f
                 bank = psum.tile([P, PAIR, 2, P], F32, name="zT_ps")
                 for i in range(PAIR):
                     for u in range(2):
-                        if pair == 0:
-                            nc.tensor.transpose(bank[:, i, u, :], z_words[:, i, u:WORDS:2], ident[:])
-                        else:
-                            nc.tensor.transpose(bank[:, i, u, :], z_sorted[r][:, i, u, :], ident[:])
+                        nc.tensor.transpose(bank[:, i, u, :], z_words[:, pair * PAIR + i, u:WORDS:2], ident[:])
                 zT_ps[r].append(bank)
+
+        def hidden_leaves_psum(r):
+            nc.vector.tensor_copy(out=hT_sb[r][:, SECOND_PAIR, :], in_=hT_ps[r][:, SECOND_PAIR, :])
 
         def leave_psum(r):
             hT_sb[r] = work.tile([P, ROUND, P], F32, name="hT_sb")
-            nc.scalar.copy(out=hT_sb[r][:], in_=hT_ps[r][:])
+            nc.scalar.copy(out=hT_sb[r][:, FIRST_PAIR, :], in_=hT_ps[r][:, FIRST_PAIR, :])
             grouped[r] = []
             for pair in range(PAIRS):
                 values = work.tile([P, PAIR, P, 4], BF16, name="grouped", align_bytes=64)
@@ -224,7 +217,6 @@ def tile_treelstm_pa_t_kernel(tc, z_node, z_children, W_f_words, W_f_scales, U_f
         )
         bias = b_rows[:].unsqueeze(1).to_broadcast([P, PAIR, CH])
 
-        sort_words(0)
         for step in range(-2, ROUNDS + 4):
             run(load, step + 6)
             run(quantise, step + 1)
@@ -237,4 +229,4 @@ def tile_treelstm_pa_t_kernel(tc, z_node, z_children, W_f_words, W_f_scales, U_f
             run(add_terms, step)
             if step - 1 == ROUNDS - 2:
                 weigh(nc.vector, step - 1, SECOND_PAIR)
-            run(sort_words, step + 3)
+            run(hidden_leaves_psum, step + 2)

@@ -14,19 +14,43 @@ SIGMOID = mybir.ActivationFunctionType.Sigmoid
 
 P = 128
 NODES, CHILDREN, SIZE, CH = 512, 32, 512, 256
-ROUND = 4
 PAIR = 2
-PAIRS = ROUND // PAIR
-ROUNDS_PER_TILE = CHILDREN // ROUND
-ROUNDS = (NODES // P) * ROUNDS_PER_TILE
-FIRST_PAIR, SECOND_PAIR, WHOLE_ROUND = slice(0, PAIR), slice(PAIR, ROUND), slice(0, ROUND)
+ROUND = 4
 WORDS = SIZE // 2
+TILES = NODES // P
+HEAD, TAIL, SORT_S, PAIRS_SQ, VTAIL, VOUT = [2, 2], [4], 0, 0, 3, 0
+H_V, SORTPOS, BQ, ADDORD, SUMLAG, VM = 1, "end", "sync", 0, 2, 0
+PE = "p0 p1 m p2 p3 T S h z0 z1"
+QPOS = "start"
+LOADORD = "u"
+VADD, VAPOS = 0, 0
+HEAD = [2,2]
+TAIL = [4]
+SUMLAG = 3
+H_V = 0
+VM = 1
+VADD = 1
 
 FLOPS = 2 * NODES * CHILDREN * CH * (SIZE + CH)
 
 
+def round_list():
+    rounds = []
+    for tile in range(TILES):
+        head = HEAD if tile == 0 else []
+        tail = TAIL if tile == TILES - 1 else []
+        sizes = head + [ROUND] * ((CHILDREN - sum(head) - sum(tail)) // ROUND) + tail
+        kid = 0
+        for n in sizes:
+            rounds.append((tile, kid, n, kid == 0, kid + n == CHILDREN))
+            kid += n
+    return rounds
+
+
 def tile_treelstm_pa_t_kernel(tc, z_node, z_children, W_f_words, W_f_scales, U_f, b_f, out):
     nc = tc.nc
+    rounds = round_list()
+    ROUNDS = len(rounds)
     with (
         tc.tile_pool(name="const", bufs=1) as const,
         tc.tile_pool(name="loads", bufs=4) as loads,
@@ -34,40 +58,59 @@ def tile_treelstm_pa_t_kernel(tc, z_node, z_children, W_f_words, W_f_scales, U_f
         tc.psum_pool(name="psum", bufs=2) as psum,
         tc.manual_schedule(),
     ):
-        z_in, zc_in, zT_ps, hT_ps, z_codes, z_scales, hT_sb = {}, {}, {}, {}, {}, {}, {}
-        grouped, mx_ps, hu_ps, gate, gated, sumsT_ps, sumsT_sb = {}, {}, {}, {}, {}, {}, {}
+        z_in, zc_in, zT_ps, hT_ps, z_codes, z_scales, hT_sb, zs = {}, {}, {}, {}, {}, {}, {}, {}
+        grouped, mx_ps, hu_ps, gate, gated, sumsT_ps, sumsT_sb, turned = {}, {}, {}, {}, {}, {}, {}, {}
 
         def load(r):
-            node_tile, j = divmod(r, ROUNDS_PER_TILE)
-            rows = slice(node_tile * P, (node_tile + 1) * P)
-            kids = slice(j * ROUND, (j + 1) * ROUND)
-            zc_in[r] = loads.tile([P, ROUND, SIZE], BF16, name="zc_in", bufs=8)
+            tile, kid, n, is_first, is_last = rounds[r]
+            rows = slice(tile * P, (tile + 1) * P)
+            kids = slice(kid, kid + n)
+            zc_in[r] = loads.tile([P, n, SIZE], BF16, name="zc_in", bufs=8)
             nc.sync.dma_start(out=zc_in[r][:], in_=z_children[rows, kids, :])
-            z_in[r] = loads.tile([P, ROUND, SIZE], BF16, name="z_in", bufs=6)
+            z_in[r] = loads.tile([P, n, SIZE], BF16, name="z_in", bufs=6)
             nc.sync.dma_start(out=z_in[r][:], in_=z_node[rows, kids, :])
 
-        def transpose(r):
-            hT_ps[r] = psum.tile([P, ROUND, P], F32, name="hT_ps", bufs=1)
+        def sort(r):
+            k = min(SORT_S, rounds[r][2])
+            if k:
+                zs[r] = work.tile([P, k, 2, P], F32, name="zs")
+                zw = z_in[r][:].bitcast(F32).rearrange("p i (w u) -> p i u w", u=2)
+                nc.scalar.copy(out=zs[r][:], in_=zw[:, 0:k])
+
+        def transpose_h(r):
+            n = rounds[r][2]
+            hT_ps[r] = psum.tile([P, n, P], F32, name="hT_ps", bufs=1)
             zc_words = zc_in[r][:].bitcast(F32)
-            for i in range(ROUND):
+            for i in range(n):
                 nc.tensor.transpose(hT_ps[r][:, i, :], zc_words[:, i, 0 : CH // 2], ident[:])
+
+        def transpose_z(r, pair):
             z_words = z_in[r][:].bitcast(F32)
-            zT_ps[r] = []
-            for pair in range(PAIRS):
+            if pair == 0:
+                zT_ps[r] = []
+            if pair < rounds[r][2] // PAIR:
                 bank = psum.tile([P, PAIR, 2, P], F32, name="zT_ps")
                 for i in range(PAIR):
                     for u in range(2):
-                        nc.tensor.transpose(bank[:, i, u, :], z_words[:, pair * PAIR + i, u:WORDS:2], ident[:])
+                        k = pair * PAIR + i
+                        src = zs[r][:, k, u, :] if k < SORT_S else z_words[:, k, u:WORDS:2]
+                        nc.tensor.transpose(bank[:, i, u, :], src, ident[:])
                 zT_ps[r].append(bank)
 
         def hidden_leaves_psum(r):
-            nc.vector.tensor_copy(out=hT_sb[r][:, SECOND_PAIR, :], in_=hT_ps[r][:, SECOND_PAIR, :])
+            n = rounds[r][2]
+            if H_V and n == ROUND:
+                sl = slice(4 - 2 * H_V, 4)
+                nc.vector.tensor_copy(out=hT_sb[r][:, sl, :], in_=hT_ps[r][:, sl, :])
 
         def leave_psum(r):
-            hT_sb[r] = work.tile([P, ROUND, P], F32, name="hT_sb")
-            nc.scalar.copy(out=hT_sb[r][:, FIRST_PAIR, :], in_=hT_ps[r][:, FIRST_PAIR, :])
+            n = rounds[r][2]
+            hT_sb[r] = work.tile([P, n, P], F32, name="hT_sb")
+            k = n - 2 * H_V if n == ROUND else n
+            if k:
+                nc.scalar.copy(out=hT_sb[r][:, 0:k, :], in_=hT_ps[r][:, 0:k, :])
             grouped[r] = []
-            for pair in range(PAIRS):
+            for pair in range(n // PAIR):
                 values = work.tile([P, PAIR, P, 4], BF16, name="grouped", align_bytes=64)
                 nc.scalar.copy(out=values[:].bitcast(F32), in_=zT_ps[r][pair][:].rearrange("p i u b -> p i b u"))
                 grouped[r].append(values)
@@ -75,9 +118,9 @@ def tile_treelstm_pa_t_kernel(tc, z_node, z_children, W_f_words, W_f_scales, U_f
         def quantise(r):
             z_codes[r] = []
             z_scales[r] = []
-            for pair in range(PAIRS):
-                codes = work.tile([P, PAIR * P], U32, align_bytes=64)
-                scales = work.tile([P, PAIR * P], U8, align_bytes=64)
+            for pair in range(rounds[r][2] // PAIR):
+                codes = work.tile([P, PAIR * P], U32, name="codes", align_bytes=64)
+                scales = work.tile([P, PAIR * P], U8, name="scales", align_bytes=64)
                 nc.vector.quantize_mx(
                     out=codes[:].bitcast(FP8X4),
                     scales=scales[:],
@@ -86,25 +129,29 @@ def tile_treelstm_pa_t_kernel(tc, z_node, z_children, W_f_words, W_f_scales, U_f
                 z_codes[r].append(codes)
                 z_scales[r].append(scales)
 
-        def multiply_plain(r, pair):
+        def multiply_plain(r, child):
+            if child >= rounds[r][2]:
+                return
             hT = hT_sb[r][:].bitcast(BF16).rearrange("p i (b e) -> p i b e", e=2)
-            bank = psum.tile([P, PAIR, CH], F32, name="hu_ps")
-            for i in range(PAIR):
-                for e in range(2):
-                    nc.tensor.matmul(
-                        bank[:, i, :],
-                        lhsT=hT[:, pair * PAIR + i, :, e],
-                        rhs=uT[:, e, :],
-                        start=(e == 0),
-                        stop=(e == 1),
-                    )
-            hu_ps[r].append(bank)
+            pair, i = divmod(child, PAIR)
+            if child == 0:
+                hu_ps[r] = []
+            if i == 0:
+                hu_ps[r].append(psum.tile([P, PAIR, CH], F32, name="hu_ps"))
+            bank = hu_ps[r][pair]
+            for e in range(2):
+                nc.tensor.matmul(
+                    bank[:, i, :],
+                    lhsT=hT[:, child, :, e],
+                    rhs=uT[:, e, :],
+                    start=(e == 0),
+                    stop=(e == 1),
+                )
 
-        def multiply(r):
-            hu_ps[r] = []
-            multiply_plain(r, 0)
+        def multiply_mx(r):
+            n = rounds[r][2]
             mx_ps[r] = []
-            for pair in range(PAIRS):
+            for pair in range(n // PAIR):
                 bank = psum.tile([P, PAIR, CH], F32, name="mx_ps")
                 for i in range(PAIR):
                     nc.tensor.matmul_mx(
@@ -117,16 +164,22 @@ def tile_treelstm_pa_t_kernel(tc, z_node, z_children, W_f_words, W_f_scales, U_f
                         stop=True,
                     )
                 mx_ps[r].append(bank)
-            multiply_plain(r, 1)
 
         def add_terms(r):
-            gate[r] = work.tile([P, ROUND, CH], F32, name="gate")
+            n = rounds[r][2]
+            gate[r] = work.tile([P, n, CH], F32, name="gate")
             first = gate[r][:, 0:PAIR, :]
+            if n == PAIR:
+                nc.vector.tensor_tensor(out=first, in0=hu_ps[r][0][:], in1=bias, op=ADD)
+                nc.vector.tensor_tensor(out=first, in0=mx_ps[r][0][:], in1=first, op=ADD)
+                return
             second = gate[r][:, PAIR:ROUND, :]
-            nc.vector.tensor_tensor(out=first, in0=hu_ps[r][0][:], in1=bias, op=ADD)
-            nc.vector.tensor_tensor(out=second, in0=mx_ps[r][1][:], in1=bias, op=ADD)
-            nc.vector.tensor_tensor(out=first, in0=mx_ps[r][0][:], in1=first, op=ADD)
-            nc.vector.tensor_tensor(out=second, in0=hu_ps[r][1][:], in1=second, op=ADD)
+            h0, h1, m0, m1 = hu_ps[r][0][:], hu_ps[r][1][:], mx_ps[r][0][:], mx_ps[r][1][:]
+            seq = {0: [(first, h0, 0), (second, m1, 0), (first, m0, 1), (second, h1, 1)],
+                   1: [(first, h0, 0), (first, m0, 1), (second, m1, 0), (second, h1, 1)],
+                   2: [(first, m0, 0), (second, m1, 0), (first, h0, 1), (second, h1, 1)]}[ADDORD]
+            for o, ps, acc in seq:
+                nc.vector.tensor_tensor(out=o, in0=ps, in1=o if acc else bias, op=ADD)
 
         def squash(r, kids):
             nc.scalar.activation(out=gate[r][:, kids, :], in_=gate[r][:, kids, :], func=SIGMOID)
@@ -134,65 +187,121 @@ def tile_treelstm_pa_t_kernel(tc, z_node, z_children, W_f_words, W_f_scales, U_f
         def weigh(engine, r, kids):
             engine.tensor_tensor(out=gated[r][:, kids, :], in0=gate[r][:, kids, :], in1=zc_in[r][:, kids, CH:SIZE], op=MULT)
 
+        def pair_index(r):
+            return sum(x[2] for x in rounds[r:]) // PAIR
+
         def squash_and_weigh(r):
-            gated[r] = work.tile([P, ROUND, CH], F32, name="gated")
-            if r == ROUNDS - 1:
-                for kids in (FIRST_PAIR, SECOND_PAIR):
+            n = rounds[r][2]
+            gated[r] = work.tile([P, n, CH], F32, name="gated")
+            late = [pair_index(r) - p <= VTAIL for p in range(n // PAIR)]
+            if VOUT and r == ROUNDS - 1:
+                late = [True] * (n // PAIR)
+            if r == ROUNDS - 1 or PAIRS_SQ:
+                for p in range(n // PAIR):
+                    kids = slice(p * PAIR, p * PAIR + PAIR)
                     squash(r, kids)
-                    weigh(nc.vector, r, kids)
-            elif r == ROUNDS - 2:
-                squash(r, WHOLE_ROUND)
-                weigh(nc.gpsimd, r, FIRST_PAIR)
+                    if not late[p]:
+                        weigh(nc.gpsimd, r, kids)
+                    elif r == ROUNDS - 1:
+                        weigh(nc.vector, r, kids)
             else:
-                squash(r, WHOLE_ROUND)
-                weigh(nc.gpsimd, r, WHOLE_ROUND)
+                squash(r, slice(0, n))
+                m = sum(1 for x in late if not x) * PAIR
+                if m == ROUND:
+                    m -= VM
+                if m:
+                    weigh(nc.gpsimd, r, slice(0, m))
+
+        def pre_add(r):
+            if VADD and rounds[r][2] == ROUND and pair_index(r) - 1 > VTAIL:
+                lo = 0
+                nc.vector.tensor_tensor(
+                    out=gated[r][:, lo : lo + VADD, :],
+                    in0=gated[r][:, lo : lo + VADD, :],
+                    in1=gated[r][:, ROUND - VADD : ROUND, :],
+                    op=ADD,
+                )
+
+        def weigh_late(r):
+            n = rounds[r][2]
+            if r == ROUNDS - 1:
+                return
+            if VM and n == ROUND and pair_index(r) - 1 > VTAIL:
+                weigh(nc.vector, r, slice(ROUND - VM, ROUND))
+            for p in range(n // PAIR):
+                if pair_index(r) - p <= VTAIL:
+                    weigh(nc.vector, r, slice(p * PAIR, p * PAIR + PAIR))
 
         def add_up(r):
-            node_tile, j = divmod(r, ROUNDS_PER_TILE)
-            if j == 0:
-                sumsT_ps[node_tile] = psum.tile([P, 2, P], F32, name="sumsT_ps", bufs=1)
-            for i in range(ROUND):
+            tile, kid, n, first, last = rounds[r]
+            if VOUT:
+                if r == ROUNDS - 1:
+                    return
+                last = last or r == ROUNDS - 2
+            if first:
+                sumsT_ps[tile] = psum.tile([P, 2, P], F32, name="sumsT_ps", bufs=1)
+            if VADD and n == ROUND and pair_index(r) - 1 > VTAIL:
+                n = n - VADD
+            for i in range(n):
                 for a in range(2):
                     nc.tensor.matmul(
-                        sumsT_ps[node_tile][:, a, :],
+                        sumsT_ps[tile][:, a, :],
                         lhsT=gated[r][:, i, a * P : (a + 1) * P],
                         rhs=ident[:],
                         is_transpose=True,
-                        start=(j == 0 and i == 0 and a == 0),
-                        stop=(j == ROUNDS_PER_TILE - 1 and i == ROUND - 1 and a == 1),
+                        start=(first and i == 0 and a == 0),
+                        stop=(last and i == n - 1 and a == 1),
                     )
-            if j == ROUNDS_PER_TILE - 1:
-                sumsT_sb[node_tile] = work.tile([P, 2, P], F32, name="sumsT_sb", bufs=2)
-                nc.scalar.copy(out=sumsT_sb[node_tile][:], in_=sumsT_ps[node_tile][:])
+            if last:
+                sumsT_sb[tile] = work.tile([P, 2, P], F32, name="sumsT_sb", bufs=2)
+                nc.scalar.copy(out=sumsT_sb[tile][:], in_=sumsT_ps[tile][:])
 
         def store(r):
-            node_tile, j = divmod(r, ROUNDS_PER_TILE)
-            if j == ROUNDS_PER_TILE - 1:
+            tile, kid, n, first, last = rounds[r]
+            if VOUT and r == ROUNDS - 2:
+                turned[tile] = psum.tile([P, ROUND, P], F32, name="hT_ps", bufs=1)
+                for a in range(2):
+                    nc.tensor.transpose(turned[tile][:, a, :], sumsT_sb[tile][:, a, :], ident[:])
+                return
+            if not last:
+                return
+            out_sb = work.tile([P, 2, P], F32, name="out_sb", bufs=2)
+            if VOUT and r == ROUNDS - 1:
+                flat = out_sb[:].rearrange("p a c -> p (a c)")
+                nc.vector.tensor_tensor(out=flat, in0=turned[tile][:, 0:2, :].rearrange("p a c -> p (a c)"), in1=gated[r][:, 0, :], op=ADD)
+                for i in range(1, n):
+                    nc.vector.tensor_tensor(out=flat, in0=flat, in1=gated[r][:, i, :], op=ADD)
+            else:
                 sums_ps = psum.tile([P, ROUND, P], F32, name="hT_ps", bufs=1)
                 for a in range(2):
-                    nc.tensor.transpose(sums_ps[:, a, :], sumsT_sb[node_tile][:, a, :], ident[:])
-                out_sb = work.tile([P, 2, P], F32, bufs=2)
+                    nc.tensor.transpose(sums_ps[:, a, :], sumsT_sb[tile][:, a, :], ident[:])
                 nc.scalar.copy(out=out_sb[:], in_=sums_ps[:, 0:2, :])
-                nc.sync.dma_start(
-                    out=out[node_tile * P : (node_tile + 1) * P, :], in_=out_sb[:].rearrange("p a c -> p (a c)")
-                )
+            nc.sync.dma_start(
+                out=out[tile * P : (tile + 1) * P, :], in_=out_sb[:].rearrange("p a c -> p (a c)")
+            )
 
         def run(stage, r):
             if 0 <= r < ROUNDS:
                 stage(r)
 
-        warm = const.tile([P, 2], F32)
+        warm = const.tile([P, 2], F32, name="warm")
         nc.vector.memset(warm[:], 0.0)
         nc.scalar.activation(out=warm[:, 1:2], in_=warm[:, 0:1], func=SIGMOID)
-        ident = const.tile([P, P], F32)
+        ident = const.tile([P, P], F32, name="ident")
         make_identity(nc, ident[:])
-        w_scales = const.tile([P, CH], U8, align_bytes=64)
+        w_scales = const.tile([P, CH], U8, name="w_scales", align_bytes=64)
         nc.vector.memset(w_scales[:].bitcast(I32), 0)
 
-        u_rows = const.tile([P, 2, CH], BF16)
-        nc.sync.dma_start(out=u_rows[:], in_=U_f.rearrange("(a p) k -> p a k", p=P))
-        load(0)
-        w_codes = const.tile([P, 2 * CH], U8, align_bytes=64)
+        u_rows = const.tile([P, 2, CH], BF16, name="u_rows")
+        b_rows = const.tile([P, CH], BF16, name="b_rows")
+        w_codes = const.tile([P, 2 * CH], U8, name="w_codes", align_bytes=64)
+        ubq = nc.scalar if BQ == "scalar" else nc.sync
+        if LOADORD == "u":
+            ubq.dma_start(out=u_rows[:], in_=U_f.rearrange("(a p) k -> p a k", p=P))
+            load(0)
+        else:
+            load(0)
+            ubq.dma_start(out=u_rows[:], in_=U_f.rearrange("(a p) k -> p a k", p=P))
         nc.sync.dma_start(out=w_codes[:].bitcast(I32), in_=W_f_words[0].bitcast(I32))
         for quadrant in range(4):
             nc.sync.dma_start(
@@ -200,33 +309,51 @@ def tile_treelstm_pa_t_kernel(tc, z_node, z_children, W_f_words, W_f_scales, U_f
                 in_=W_f_scales[0, 4 * quadrant : 4 * quadrant + 4, :].bitcast(I32),
             )
         load(1)
-        b_rows = const.tile([P, CH], BF16)
-        nc.sync.dma_start(out=b_rows[:], in_=b_f.partition_broadcast(P))
+        ubq.dma_start(out=b_rows[:], in_=b_f.partition_broadcast(P))
         load(2)
         load(3)
 
         u_ps = psum.tile([P, ROUND, P], F32, name="hT_ps", bufs=1)
         for a in range(2):
             nc.tensor.transpose(u_ps[:, a, :], u_rows[:].bitcast(F32)[:, a, :], ident[:])
-        uT_words = const.tile([P, 2, P], F32)
+        uT_words = const.tile([P, 2, P], F32, name="uT_words")
         nc.vector.tensor_copy(out=uT_words[:], in_=u_ps[:, 0:2, :])
-        uT = const.tile([P, 2, CH], BF16)
+        uT = const.tile([P, 2, CH], BF16, name="uT")
         nc.vector.tensor_copy(
             out=uT[:].rearrange("p e (a c) -> p e a c", a=2),
             in_=uT_words[:].bitcast(BF16).rearrange("p a (c e) -> p e a c", e=2),
         )
         bias = b_rows[:].unsqueeze(1).to_broadcast([P, PAIR, CH])
 
-        for step in range(-2, ROUNDS + 4):
-            run(load, step + 6)
-            run(quantise, step + 1)
+        for step in range(-3, ROUNDS + SUMLAG + 2):
+            if step > -3:
+                run(load, step + 6)
+            if QPOS == "start":
+                run(quantise, step + 1)
             run(squash_and_weigh, step - 1)
-            run(multiply, step)
-            run(store, step - 3)
-            run(add_up, step - 2)
-            run(transpose, step + 2)
+            for word in PE.split():
+                if word[0] == "p":
+                    if 0 <= step < ROUNDS:
+                        multiply_plain(step, int(word[1]))
+                elif word == "m":
+                    run(multiply_mx, step)
+                elif word == "T":
+                    run(store, step - SUMLAG - 1)
+                elif word == "S":
+                    run(add_up, step - SUMLAG)
+                elif word == "h":
+                    run(transpose_h, step + 2)
+                elif word[0] == "z":
+                    if 0 <= step + 2 < ROUNDS:
+                        transpose_z(step + 2, int(word[1]))
             run(leave_psum, step + 2)
             run(add_terms, step)
-            if step - 1 == ROUNDS - 2:
-                weigh(nc.vector, step - 1, SECOND_PAIR)
+            if VAPOS == 0:
+                run(pre_add, step - 2)
+            run(weigh_late, step - 1)
+            if VAPOS == 1:
+                run(pre_add, step - 2)
             run(hidden_leaves_psum, step + 2)
+            if QPOS == "end":
+                run(quantise, step + 2)
+            run(sort, step + 3)

@@ -23,13 +23,19 @@ H_V, SORTPOS, BQ, ADDORD, SUMLAG, VM = 1, "end", "sync", 0, 2, 0
 PE = "p0 p1 m p2 p3 T S h z0 z1"
 QPOS = "start"
 LOADORD = "u"
-VADD, VAPOS = 0, 0
+GADD, MXREV, SB, GW = 0, 0, 1, 0
+ROT = {}
+WT = 4
+SO, SQD, VPRE, VPOST = "", 1, "q", "+ m"
+VADD, VAPOS, QW, TRL, DADD = 0, 0, 0, 2, 0
 HEAD = [2,2]
 TAIL = [4]
 SUMLAG = 3
 H_V = 0
 VM = 1
 VADD = 1
+WT = 10
+ROT = {"mx0":"mx1","mx1":"mx0","hu1":"h","h":"hu1"}
 
 FLOPS = 2 * NODES * CHILDREN * CH * (SIZE + CH)
 
@@ -61,11 +67,21 @@ def tile_treelstm_pa_t_kernel(tc, z_node, z_children, W_f_words, W_f_scales, U_f
         z_in, zc_in, zT_ps, hT_ps, z_codes, z_scales, hT_sb, zs = {}, {}, {}, {}, {}, {}, {}, {}
         grouped, mx_ps, hu_ps, gate, gated, sumsT_ps, sumsT_sb, turned = {}, {}, {}, {}, {}, {}, {}, {}
 
+        owner = {"hu0": "bank0", "mx0": "bank1", "mx1": "bank2", "hu1": "bank3", "h": "bank4"}
+
+        def bank_tile(shape, role):
+            return psum.tile(shape, F32, name=owner[role], bufs=1)
+
+        def rotate():
+            old = dict(owner)
+            for role, source in ROT.items():
+                owner[role] = old[source]
+
         def load(r):
             tile, kid, n, is_first, is_last = rounds[r]
             rows = slice(tile * P, (tile + 1) * P)
             kids = slice(kid, kid + n)
-            zc_in[r] = loads.tile([P, n, SIZE], BF16, name="zc_in", bufs=8)
+            zc_in[r] = loads.tile([P, n, SIZE], BF16, name="zc_in", bufs=TRL + 6)
             nc.sync.dma_start(out=zc_in[r][:], in_=z_children[rows, kids, :])
             z_in[r] = loads.tile([P, n, SIZE], BF16, name="z_in", bufs=6)
             nc.sync.dma_start(out=z_in[r][:], in_=z_node[rows, kids, :])
@@ -79,7 +95,7 @@ def tile_treelstm_pa_t_kernel(tc, z_node, z_children, W_f_words, W_f_scales, U_f
 
         def transpose_h(r):
             n = rounds[r][2]
-            hT_ps[r] = psum.tile([P, n, P], F32, name="hT_ps", bufs=1)
+            hT_ps[r] = bank_tile([P, n, P], "h")
             zc_words = zc_in[r][:].bitcast(F32)
             for i in range(n):
                 nc.tensor.transpose(hT_ps[r][:, i, :], zc_words[:, i, 0 : CH // 2], ident[:])
@@ -104,20 +120,77 @@ def tile_treelstm_pa_t_kernel(tc, z_node, z_children, W_f_words, W_f_scales, U_f
                 nc.vector.tensor_copy(out=hT_sb[r][:, sl, :], in_=hT_ps[r][:, sl, :])
 
         def leave_psum(r):
+            leave_h(r)
+            leave_z0(r)
+            leave_z1(r)
+
+        def squash_a(r):
+            squash(r, slice(0, PAIR))
+
+        def squash_b(r):
+            if rounds[r][2] > PAIR:
+                squash(r, slice(PAIR, ROUND))
+
+        def weigh_early(r):
             n = rounds[r][2]
-            hT_sb[r] = work.tile([P, n, P], F32, name="hT_sb")
+            gated[r] = work.tile([P, n, CH], F32, name="gated", bufs=SUMLAG + 1 + SB)
+            late = [pair_index(r) - p <= VTAIL for p in range(n // PAIR)]
+            if r == ROUNDS - 1:
+                for p in range(n // PAIR):
+                    kids = slice(p * PAIR, p * PAIR + PAIR)
+                    weigh(nc.vector if late[p] else nc.gpsimd, r, kids)
+                return
+            m = sum(1 for x in late if not x) * PAIR
+            if m == ROUND and pair_index(r) > WT:
+                m -= VM
+            if m:
+                weigh(nc.gpsimd, r, slice(0, m))
+
+        def leave_z0(r):
+            leave_z(r, 0)
+
+        def leave_z1(r):
+            if rounds[r][2] > PAIR:
+                leave_z(r, 1)
+
+        def leave_h(r):
+            n = rounds[r][2]
+            hT_sb[r] = work.tile([P, n, P], F32, name="hT_sb", bufs=TRL + 2)
             k = n - 2 * H_V if n == ROUND else n
             if k:
                 nc.scalar.copy(out=hT_sb[r][:, 0:k, :], in_=hT_ps[r][:, 0:k, :])
-            grouped[r] = []
-            for pair in range(n // PAIR):
-                values = work.tile([P, PAIR, P, 4], BF16, name="grouped", align_bytes=64)
-                nc.scalar.copy(out=values[:].bitcast(F32), in_=zT_ps[r][pair][:].rearrange("p i u b -> p i b u"))
+
+        def leave_z(r, pair):
+            n = rounds[r][2]
+            if pair == 0:
+                grouped[r] = []
+            if QW and pair == 0:
+                grouped[r].append(work.tile([P, n, P, 4], BF16, name="grouped", bufs=TRL + 2, align_bytes=64))
+            if QW:
+                half = grouped[r][0][:, pair * PAIR : pair * PAIR + PAIR]
+            else:
+                values = work.tile([P, PAIR, P, 4], BF16, name="grouped", bufs=2 * TRL, align_bytes=64)
+                half = values[:]
                 grouped[r].append(values)
+            nc.scalar.copy(out=half.bitcast(F32), in_=zT_ps[r][pair][:].rearrange("p i u b -> p i b u"))
 
         def quantise(r):
             z_codes[r] = []
             z_scales[r] = []
+            if QW:
+                n = rounds[r][2]
+                codes = work.tile([P, n * P], U32, name="codes", align_bytes=64)
+                scales = work.tile([P, n * P], U8, name="scales", align_bytes=64)
+                nc.vector.quantize_mx(
+                    out=codes[:].bitcast(FP8X4),
+                    scales=scales[:],
+                    in_=grouped[r][0][:].rearrange("p i b t -> p (i b t)"),
+                )
+                for pair in range(n // PAIR):
+                    cols = slice(pair * PAIR * P, (pair + 1) * PAIR * P)
+                    z_codes[r].append(codes[:, cols])
+                    z_scales[r].append(scales[:, cols])
+                return
             for pair in range(rounds[r][2] // PAIR):
                 codes = work.tile([P, PAIR * P], U32, name="codes", align_bytes=64)
                 scales = work.tile([P, PAIR * P], U8, name="scales", align_bytes=64)
@@ -137,7 +210,7 @@ def tile_treelstm_pa_t_kernel(tc, z_node, z_children, W_f_words, W_f_scales, U_f
             if child == 0:
                 hu_ps[r] = []
             if i == 0:
-                hu_ps[r].append(psum.tile([P, PAIR, CH], F32, name="hu_ps"))
+                hu_ps[r].append(bank_tile([P, PAIR, CH], "hu%d" % pair))
             bank = hu_ps[r][pair]
             for e in range(2):
                 nc.tensor.matmul(
@@ -150,9 +223,9 @@ def tile_treelstm_pa_t_kernel(tc, z_node, z_children, W_f_words, W_f_scales, U_f
 
         def multiply_mx(r):
             n = rounds[r][2]
-            mx_ps[r] = []
-            for pair in range(n // PAIR):
-                bank = psum.tile([P, PAIR, CH], F32, name="mx_ps")
+            mx_ps[r] = {}
+            for pair in reversed(range(n // PAIR)) if MXREV else range(n // PAIR):
+                bank = bank_tile([P, PAIR, CH], "mx%d" % pair)
                 for i in range(PAIR):
                     nc.tensor.matmul_mx(
                         out=bank[:, i, :],
@@ -163,7 +236,7 @@ def tile_treelstm_pa_t_kernel(tc, z_node, z_children, W_f_words, W_f_scales, U_f
                         start=True,
                         stop=True,
                     )
-                mx_ps[r].append(bank)
+                mx_ps[r][pair] = bank
 
         def add_terms(r):
             n = rounds[r][2]
@@ -177,7 +250,10 @@ def tile_treelstm_pa_t_kernel(tc, z_node, z_children, W_f_words, W_f_scales, U_f
             h0, h1, m0, m1 = hu_ps[r][0][:], hu_ps[r][1][:], mx_ps[r][0][:], mx_ps[r][1][:]
             seq = {0: [(first, h0, 0), (second, m1, 0), (first, m0, 1), (second, h1, 1)],
                    1: [(first, h0, 0), (first, m0, 1), (second, m1, 0), (second, h1, 1)],
-                   2: [(first, m0, 0), (second, m1, 0), (first, h0, 1), (second, h1, 1)]}[ADDORD]
+                   2: [(first, m0, 0), (second, m1, 0), (first, h0, 1), (second, h1, 1)],
+                   3: [(second, m1, 0), (first, h0, 0), (first, m0, 1), (second, h1, 1)],
+                   4: [(second, m1, 0), (first, m0, 0), (first, h0, 1), (second, h1, 1)],
+                   5: [(second, m1, 0), (first, m0, 0), (second, h1, 1), (first, h0, 1)]}[ADDORD]
             for o, ps, acc in seq:
                 nc.vector.tensor_tensor(out=o, in0=ps, in1=o if acc else bias, op=ADD)
 
@@ -190,9 +266,15 @@ def tile_treelstm_pa_t_kernel(tc, z_node, z_children, W_f_words, W_f_scales, U_f
         def pair_index(r):
             return sum(x[2] for x in rounds[r:]) // PAIR
 
+        def open_window(r):
+            gated[r] = work.tile([P, rounds[r][2], CH], F32, name="gated", bufs=SUMLAG + 1 + SB)
+            if r < ROUNDS - 1 and pair_index(r) > VTAIL:
+                nc.vector.memset(gated[r][:, 0, 0:1], 0.0)
+
         def squash_and_weigh(r):
             n = rounds[r][2]
-            gated[r] = work.tile([P, n, CH], F32, name="gated")
+            if not GW:
+                gated[r] = work.tile([P, n, CH], F32, name="gated", bufs=SUMLAG + 1 + SB)
             late = [pair_index(r) - p <= VTAIL for p in range(n // PAIR)]
             if VOUT and r == ROUNDS - 1:
                 late = [True] * (n // PAIR)
@@ -207,13 +289,15 @@ def tile_treelstm_pa_t_kernel(tc, z_node, z_children, W_f_words, W_f_scales, U_f
             else:
                 squash(r, slice(0, n))
                 m = sum(1 for x in late if not x) * PAIR
-                if m == ROUND:
+                if m == ROUND and pair_index(r) > WT:
                     m -= VM
                 if m:
                     weigh(nc.gpsimd, r, slice(0, m))
+                if GADD and n == ROUND and pair_index(r) > WT:
+                    nc.gpsimd.tensor_tensor(out=gated[r][:, 0, :], in0=gated[r][:, 0, :], in1=gated[r][:, 2, :], op=ADD)
 
         def pre_add(r):
-            if VADD and rounds[r][2] == ROUND and pair_index(r) - 1 > VTAIL:
+            if VADD and rounds[r][2] == ROUND and pair_index(r) > WT:
                 lo = 0
                 nc.vector.tensor_tensor(
                     out=gated[r][:, lo : lo + VADD, :],
@@ -222,11 +306,15 @@ def tile_treelstm_pa_t_kernel(tc, z_node, z_children, W_f_words, W_f_scales, U_f
                     op=ADD,
                 )
 
+        def dma_add(r):
+            if DADD and rounds[r][2] == ROUND and pair_index(r) > WT:
+                nc.gpsimd.dma_start(out=gated[r][:, 0:2, :], in_=gated[r][:, 2:4, :], accum_op=ADD)
+
         def weigh_late(r):
             n = rounds[r][2]
             if r == ROUNDS - 1:
                 return
-            if VM and n == ROUND and pair_index(r) - 1 > VTAIL:
+            if VM and n == ROUND and pair_index(r) > WT:
                 weigh(nc.vector, r, slice(ROUND - VM, ROUND))
             for p in range(n // PAIR):
                 if pair_index(r) - p <= VTAIL:
@@ -240,17 +328,20 @@ def tile_treelstm_pa_t_kernel(tc, z_node, z_children, W_f_words, W_f_scales, U_f
                 last = last or r == ROUNDS - 2
             if first:
                 sumsT_ps[tile] = psum.tile([P, 2, P], F32, name="sumsT_ps", bufs=1)
-            if VADD and n == ROUND and pair_index(r) - 1 > VTAIL:
-                n = n - VADD
-            for i in range(n):
+            kids = list(range(n))
+            if (VADD or DADD) and n == ROUND and pair_index(r) > WT:
+                kids = kids[: n - (VADD or 2)]
+            if GADD and n == ROUND and pair_index(r) > WT:
+                kids.remove(2)
+            for i in kids:
                 for a in range(2):
                     nc.tensor.matmul(
                         sumsT_ps[tile][:, a, :],
                         lhsT=gated[r][:, i, a * P : (a + 1) * P],
                         rhs=ident[:],
                         is_transpose=True,
-                        start=(first and i == 0 and a == 0),
-                        stop=(last and i == n - 1 and a == 1),
+                        start=(first and i == kids[0] and a == 0),
+                        stop=(last and i == kids[-1] and a == 1),
                     )
             if last:
                 sumsT_sb[tile] = work.tile([P, 2, P], F32, name="sumsT_sb", bufs=2)
@@ -259,7 +350,7 @@ def tile_treelstm_pa_t_kernel(tc, z_node, z_children, W_f_words, W_f_scales, U_f
         def store(r):
             tile, kid, n, first, last = rounds[r]
             if VOUT and r == ROUNDS - 2:
-                turned[tile] = psum.tile([P, ROUND, P], F32, name="hT_ps", bufs=1)
+                turned[tile] = bank_tile([P, ROUND, P], "h")
                 for a in range(2):
                     nc.tensor.transpose(turned[tile][:, a, :], sumsT_sb[tile][:, a, :], ident[:])
                 return
@@ -272,7 +363,7 @@ def tile_treelstm_pa_t_kernel(tc, z_node, z_children, W_f_words, W_f_scales, U_f
                 for i in range(1, n):
                     nc.vector.tensor_tensor(out=flat, in0=flat, in1=gated[r][:, i, :], op=ADD)
             else:
-                sums_ps = psum.tile([P, ROUND, P], F32, name="hT_ps", bufs=1)
+                sums_ps = bank_tile([P, ROUND, P], "h")
                 for a in range(2):
                     nc.tensor.transpose(sums_ps[:, a, :], sumsT_sb[tile][:, a, :], ident[:])
                 nc.scalar.copy(out=out_sb[:], in_=sums_ps[:, 0:2, :])
@@ -280,8 +371,11 @@ def tile_treelstm_pa_t_kernel(tc, z_node, z_children, W_f_words, W_f_scales, U_f
                 out=out[tile * P : (tile + 1) * P, :], in_=out_sb[:].rearrange("p a c -> p (a c)")
             )
 
+        done = set()
+
         def run(stage, r):
-            if 0 <= r < ROUNDS:
+            if 0 <= r < ROUNDS and (stage, r) not in done:
+                done.add((stage, r))
                 stage(r)
 
         warm = const.tile([P, 2], F32, name="warm")
@@ -313,7 +407,7 @@ def tile_treelstm_pa_t_kernel(tc, z_node, z_children, W_f_words, W_f_scales, U_f
         load(2)
         load(3)
 
-        u_ps = psum.tile([P, ROUND, P], F32, name="hT_ps", bufs=1)
+        u_ps = bank_tile([P, ROUND, P], "h")
         for a in range(2):
             nc.tensor.transpose(u_ps[:, a, :], u_rows[:].bitcast(F32)[:, a, :], ident[:])
         uT_words = const.tile([P, 2, P], F32, name="uT_words")
@@ -325,12 +419,15 @@ def tile_treelstm_pa_t_kernel(tc, z_node, z_children, W_f_words, W_f_scales, U_f
         )
         bias = b_rows[:].unsqueeze(1).to_broadcast([P, PAIR, CH])
 
-        for step in range(-3, ROUNDS + SUMLAG + 2):
-            if step > -3:
-                run(load, step + 6)
-            if QPOS == "start":
-                run(quantise, step + 1)
-            run(squash_and_weigh, step - 1)
+        for step in range(-TRL - 1, ROUNDS + SUMLAG + 4):
+            if step > -TRL - 1:
+                run(load, step + TRL + 4)
+            for word in VPRE.split():
+                run({"q": quantise, "+": pre_add, "m": weigh_late}[word], step + {"q": 1, "+": -2, "m": -1}[word])
+            if GW:
+                run(open_window, step - 1)
+            if not SO:
+                run(squash_and_weigh, step - 1)
             for word in PE.split():
                 if word[0] == "p":
                     if 0 <= step < ROUNDS:
@@ -338,22 +435,38 @@ def tile_treelstm_pa_t_kernel(tc, z_node, z_children, W_f_words, W_f_scales, U_f
                 elif word == "m":
                     run(multiply_mx, step)
                 elif word == "T":
-                    run(store, step - SUMLAG - 1)
+                    run(store, step - SUMLAG - SB)
                 elif word == "S":
-                    run(add_up, step - SUMLAG)
+                    if SB == 1:
+                        run(add_up, step - SUMLAG)
+                    elif step % 2 == 0 or step >= ROUNDS:
+                        run(add_up, step - SUMLAG - 1)
+                        run(add_up, step - SUMLAG)
                 elif word == "h":
-                    run(transpose_h, step + 2)
+                    run(transpose_h, step + TRL)
                 elif word[0] == "z":
-                    if 0 <= step + 2 < ROUNDS:
-                        transpose_z(step + 2, int(word[1]))
-            run(leave_psum, step + 2)
-            run(add_terms, step)
-            if VAPOS == 0:
-                run(pre_add, step - 2)
-            run(weigh_late, step - 1)
-            if VAPOS == 1:
-                run(pre_add, step - 2)
-            run(hidden_leaves_psum, step + 2)
-            if QPOS == "end":
-                run(quantise, step + 2)
-            run(sort, step + 3)
+                    if 0 <= step + TRL < ROUNDS:
+                        transpose_z(step + TRL, int(word[1]))
+            if SQD == 0:
+                run(add_terms, step)
+            if SO:
+                for word in SO.split():
+                    if word in ("a", "b"):
+                        run(squash_a if word == "a" else squash_b, step - SQD)
+                    elif word == "h":
+                        run(leave_h, step + TRL)
+                    else:
+                        run(leave_z0 if word == "0" else leave_z1, step + TRL)
+                run(weigh_early, step - SQD)
+            else:
+                run(leave_psum, step + TRL)
+            if "T" not in PE:
+                run(store, step - SUMLAG - SB)
+            if SQD:
+                run(add_terms, step)
+            run(dma_add, step - 2)
+            for word in VPOST.split():
+                run({"q": quantise, "+": pre_add, "m": weigh_late}[word], step + {"q": 1, "+": -2, "m": -1}[word])
+            run(hidden_leaves_psum, step + TRL)
+            rotate()
+            run(sort, step + TRL + 1)

@@ -25,6 +25,7 @@ QPOS = "start"
 LOADORD = "u"
 GADD, MXREV, SB, GW = 0, 0, 1, 0
 ROT = {}
+QMID, VMID = -1, "q"
 WT = 4
 SO, SQD, VPRE, VPOST = "", 1, "q", "+ m"
 VADD, VAPOS, QW, TRL, DADD = 0, 0, 0, 2, 0
@@ -174,9 +175,10 @@ def tile_treelstm_pa_t_kernel(tc, z_node, z_children, W_f_words, W_f_scales, U_f
                 grouped[r].append(values)
             nc.scalar.copy(out=half.bitcast(F32), in_=zT_ps[r][pair][:].rearrange("p i u b -> p i b u"))
 
-        def quantise(r):
-            z_codes[r] = []
-            z_scales[r] = []
+        def quantise(r, pairs=(0, 1)):
+            if 0 in pairs:
+                z_codes[r] = []
+                z_scales[r] = []
             if QW:
                 n = rounds[r][2]
                 codes = work.tile([P, n * P], U32, name="codes", align_bytes=64)
@@ -191,7 +193,7 @@ def tile_treelstm_pa_t_kernel(tc, z_node, z_children, W_f_words, W_f_scales, U_f
                     z_codes[r].append(codes[:, cols])
                     z_scales[r].append(scales[:, cols])
                 return
-            for pair in range(rounds[r][2] // PAIR):
+            for pair in [p for p in pairs if p < rounds[r][2] // PAIR]:
                 codes = work.tile([P, PAIR * P], U32, name="codes", align_bytes=64)
                 scales = work.tile([P, PAIR * P], U8, name="scales", align_bytes=64)
                 nc.vector.quantize_mx(
@@ -201,6 +203,12 @@ def tile_treelstm_pa_t_kernel(tc, z_node, z_children, W_f_words, W_f_scales, U_f
                 )
                 z_codes[r].append(codes)
                 z_scales[r].append(scales)
+
+        def quantise_first(r):
+            quantise(r, (0,))
+
+        def quantise_second(r):
+            quantise(r, (1,))
 
         def multiply_plain(r, child):
             if child >= rounds[r][2]:
@@ -243,6 +251,13 @@ def tile_treelstm_pa_t_kernel(tc, z_node, z_children, W_f_words, W_f_scales, U_f
             gate[r] = work.tile([P, n, CH], F32, name="gate")
             first = gate[r][:, 0:PAIR, :]
             if n == PAIR:
+                if QMID >= 0 and "b" in VMID:
+                    run(quantise_second, r + 1)
+                elif QMID >= 0:
+                    run(quantise, r + 1)
+                    run(pre_add, r - 2)
+                    run(alloc_gated, r - 1)
+                    run(weigh_late, r - 1)
                 nc.vector.tensor_tensor(out=first, in0=hu_ps[r][0][:], in1=bias, op=ADD)
                 nc.vector.tensor_tensor(out=first, in0=mx_ps[r][0][:], in1=first, op=ADD)
                 return
@@ -254,7 +269,21 @@ def tile_treelstm_pa_t_kernel(tc, z_node, z_children, W_f_words, W_f_scales, U_f
                    3: [(second, m1, 0), (first, h0, 0), (first, m0, 1), (second, h1, 1)],
                    4: [(second, m1, 0), (first, m0, 0), (first, h0, 1), (second, h1, 1)],
                    5: [(second, m1, 0), (first, m0, 0), (second, h1, 1), (first, h0, 1)]}[ADDORD]
-            for o, ps, acc in seq:
+            for k, (o, ps, acc) in enumerate(seq):
+                if k == QMID:
+                    for word in VMID.split():
+                        if word == "q":
+                            run(quantise, r + 1)
+                        elif word == "b":
+                            run(quantise_second, r + 1)
+                        elif word == "+":
+                            run(pre_add, r - 2)
+                        elif word == "m":
+                            run(alloc_gated, r - 1)
+                            run(weigh_late, r - 1)
+                        elif word == "g":
+                            run(alloc_gated, r - 1)
+                            run(open_window, r - 1)
                 nc.vector.tensor_tensor(out=o, in0=ps, in1=o if acc else bias, op=ADD)
 
         def squash(r, kids):
@@ -266,8 +295,30 @@ def tile_treelstm_pa_t_kernel(tc, z_node, z_children, W_f_words, W_f_scales, U_f
         def pair_index(r):
             return sum(x[2] for x in rounds[r:]) // PAIR
 
-        def open_window(r):
+        def alloc_gated(r):
             gated[r] = work.tile([P, rounds[r][2], CH], F32, name="gated", bufs=SUMLAG + 1 + SB)
+
+        def squash_only(r):
+            if r == ROUNDS - 1:
+                for p in range(rounds[r][2] // PAIR):
+                    squash(r, slice(p * PAIR, p * PAIR + PAIR))
+            else:
+                squash(r, slice(0, rounds[r][2]))
+
+        def weigh_g(r):
+            n = rounds[r][2]
+            late = [pair_index(r) - p <= VTAIL for p in range(n // PAIR)]
+            if r == ROUNDS - 1:
+                for p in range(n // PAIR):
+                    weigh(nc.vector if late[p] else nc.gpsimd, r, slice(p * PAIR, p * PAIR + PAIR))
+                return
+            m = sum(1 for x in late if not x) * PAIR
+            if m == ROUND and pair_index(r) > WT:
+                m -= VM
+            if m:
+                weigh(nc.gpsimd, r, slice(0, m))
+
+        def open_window(r):
             if r < ROUNDS - 1 and pair_index(r) > VTAIL:
                 nc.vector.memset(gated[r][:, 0, 0:1], 0.0)
 
@@ -387,7 +438,11 @@ def tile_treelstm_pa_t_kernel(tc, z_node, z_children, W_f_words, W_f_scales, U_f
         nc.vector.memset(w_scales[:].bitcast(I32), 0)
 
         u_rows = const.tile([P, 2, CH], BF16, name="u_rows")
-        b_rows = const.tile([P, CH], BF16, name="b_rows")
+        b_pad = const.tile([P, CH], BF16, name="b_pad")
+        nc.vector.memset(b_pad[:], 0.0)
+        ones = const.tile([P, P], BF16, name="ones")
+        nc.vector.memset(ones[:], 1.0)
+        bias_rows = const.tile([P, CH], BF16, name="bias_rows")
         w_codes = const.tile([P, 2 * CH], U8, name="w_codes", align_bytes=64)
         ubq = nc.scalar if BQ == "scalar" else nc.sync
         if LOADORD == "u":
@@ -403,7 +458,7 @@ def tile_treelstm_pa_t_kernel(tc, z_node, z_children, W_f_words, W_f_scales, U_f
                 in_=W_f_scales[0, 4 * quadrant : 4 * quadrant + 4, :].bitcast(I32),
             )
         load(1)
-        ubq.dma_start(out=b_rows[:], in_=b_f.partition_broadcast(P))
+        nc.sync.dma_start(out=b_pad[0:1, :], in_=b_f.unsqueeze(0))
         load(2)
         load(3)
 
@@ -417,16 +472,26 @@ def tile_treelstm_pa_t_kernel(tc, z_node, z_children, W_f_words, W_f_scales, U_f
             out=uT[:].rearrange("p e (a c) -> p e a c", a=2),
             in_=uT_words[:].bitcast(BF16).rearrange("p a (c e) -> p e a c", e=2),
         )
-        bias = b_rows[:].unsqueeze(1).to_broadcast([P, PAIR, CH])
+        bias = bias_rows[:].unsqueeze(1).to_broadcast([P, PAIR, CH])
+
+        def spread_bias():
+            bank = bank_tile([P, CH], "mx1")
+            nc.tensor.matmul(bank[:], lhsT=ones[:], rhs=b_pad[:], start=True, stop=True)
+            nc.vector.tensor_copy(out=bias_rows[:], in_=bank[:])
 
         for step in range(-TRL - 1, ROUNDS + SUMLAG + 4):
             if step > -TRL - 1:
                 run(load, step + TRL + 4)
+            if QMID >= 0 and step == -1 and "b" not in VMID:
+                run(quantise, 0)
             for word in VPRE.split():
-                run({"q": quantise, "+": pre_add, "m": weigh_late}[word], step + {"q": 1, "+": -2, "m": -1}[word])
-            if GW:
+                run({"q": quantise, "a": quantise_first, "+": pre_add, "m": weigh_late}[word], step + {"q": 1, "a": 1, "+": -2, "m": -1}[word])
+            if GW == 1:
+                run(alloc_gated, step - 1)
                 run(open_window, step - 1)
-            if not SO:
+            if GW == 2:
+                run(squash_only, step - 1)
+            elif not SO:
                 run(squash_and_weigh, step - 1)
             for word in PE.split():
                 if word[0] == "p":
@@ -434,6 +499,8 @@ def tile_treelstm_pa_t_kernel(tc, z_node, z_children, W_f_words, W_f_scales, U_f
                         multiply_plain(step, int(word[1]))
                 elif word == "m":
                     run(multiply_mx, step)
+                    if step == 0:
+                        spread_bias()
                 elif word == "T":
                     run(store, step - SUMLAG - SB)
                 elif word == "S":
@@ -464,9 +531,18 @@ def tile_treelstm_pa_t_kernel(tc, z_node, z_children, W_f_words, W_f_scales, U_f
                 run(store, step - SUMLAG - SB)
             if SQD:
                 run(add_terms, step)
+            if GW == 2:
+                run(alloc_gated, step - 1)
+                if step >= ROUNDS:
+                    run(weigh_late, step - 1)
+                run(weigh_g, step - 1)
+                if step >= ROUNDS:
+                    run(pre_add, step - 2)
             run(dma_add, step - 2)
+            if "b" in VMID and step < 0:
+                run(quantise_second, step + 1)
             for word in VPOST.split():
-                run({"q": quantise, "+": pre_add, "m": weigh_late}[word], step + {"q": 1, "+": -2, "m": -1}[word])
+                run({"q": quantise, "a": quantise_first, "+": pre_add, "m": weigh_late}[word], step + {"q": 1, "a": 1, "+": -2, "m": -1}[word])
             run(hidden_leaves_psum, step + TRL)
             rotate()
             run(sort, step + TRL + 1)

from concourse import mybir
from concourse.masks import make_identity

F32 = mybir.dt.float32
BF16 = mybir.dt.bfloat16
U8 = mybir.dt.uint8
U32 = mybir.dt.uint32
I32 = mybir.dt.int32
FP8X4 = mybir.dt.float8_e4m3fn_x4
FP4X4 = mybir.dt.float4_e2m1fn_x4
ADD = mybir.AluOpType.add
MULT = mybir.AluOpType.mult
SIGMOID = mybir.ActivationFunctionType.Sigmoid

P = 128
NODES, CHILDREN, SIZE, CH = 512, 32, 512, 256
PAIR = 2
ROUND = 4
WORDS = SIZE // 2
TILES = NODES // P
HEAD, TAIL, SORT_S, PAIRS_SQ, VTAIL, VOUT = [2, 2], [4], 0, 0, 3, 0
H_V, SORTPOS, BQ, ADDORD, SUMLAG, VM = 1, "end", "sync", 0, 2, 0
PE = "p0 p1 m p2 p3 T S h z0 z1"
QPOS = "start"
LOADORD = "u"
GADD, MXREV, SB, GW = 0, 0, 1, 0
ROT = {}
QMID, VMID = -1, "q"
WT = 4
SO, SQD, VPRE, VPOST = "", 1, "q", "+ m"
VADD, VAPOS, QW, TRL, DADD = 0, 0, 0, 2, 0
HEAD = [2,2]
TAIL = [4]
SUMLAG = 3
H_V = 0
VM = 1
VADD = 1
WT = 10
ROT = {"mx0":"mx1","mx1":"mx0","hu1":"h","h":"hu1"}

FLOPS = 2 * NODES * CHILDREN * CH * (SIZE + CH)


def round_list():
    rounds = []
    for tile in range(TILES):
        head = HEAD if tile == 0 else []
        tail = TAIL if tile == TILES - 1 else []
        sizes = head + [ROUND] * ((CHILDREN - sum(head) - sum(tail)) // ROUND) + tail
        kid = 0
        for n in sizes:
            rounds.append((tile, kid, n, kid == 0, kid + n == CHILDREN))
            kid += n
    return rounds


def tile_treelstm_pa_t_kernel(tc, z_node, z_children, W_f_words, W_f_scales, U_f, b_f, out):
    nc = tc.nc
    rounds = round_list()
    ROUNDS = len(rounds)
    with (
        tc.tile_pool(name="const", bufs=1) as const,
        tc.tile_pool(name="loads", bufs=4) as loads,
        tc.tile_pool(name="work", bufs=4) as work,
        tc.psum_pool(name="psum", bufs=2) as psum,
        tc.manual_schedule(),
    ):
        z_in, zc_in, zT_ps, hT_ps, z_codes, z_scales, hT_sb, zs = {}, {}, {}, {}, {}, {}, {}, {}
        grouped, mx_ps, hu_ps, gate, gated, sumsT_ps, sumsT_sb, turned = {}, {}, {}, {}, {}, {}, {}, {}

        owner = {"hu0": "bank0", "mx0": "bank1", "mx1": "bank2", "hu1": "bank3", "h": "bank4"}

        def bank_tile(shape, role):
            return psum.tile(shape, F32, name=owner[role], bufs=1)

        def rotate():
            old = dict(owner)
            for role, source in ROT.items():
                owner[role] = old[source]

        def load(r):
            tile, kid, n, is_first, is_last = rounds[r]
            rows = slice(tile * P, (tile + 1) * P)
            kids = slice(kid, kid + n)
            zc_in[r] = loads.tile([P, n, SIZE], BF16, name="zc_in", bufs=TRL + 6)
            nc.sync.dma_start(out=zc_in[r][:], in_=z_children[rows, kids, :])
            z_in[r] = loads.tile([P, n, SIZE], BF16, name="z_in", bufs=6)
            nc.sync.dma_start(out=z_in[r][:], in_=z_node[rows, kids, :])

        def sort(r):
            k = min(SORT_S, rounds[r][2])
            if k:
                zs[r] = work.tile([P, k, 2, P], F32, name="zs")
                zw = z_in[r][:].bitcast(F32).rearrange("p i (w u) -> p i u w", u=2)
                nc.scalar.copy(out=zs[r][:], in_=zw[:, 0:k])

        def transpose_h(r):
            n = rounds[r][2]
            hT_ps[r] = bank_tile([P, n, P], "h")
            zc_words = zc_in[r][:].bitcast(F32)
            for i in range(n):
                nc.tensor.transpose(hT_ps[r][:, i, :], zc_words[:, i, 0 : CH // 2], ident[:])

        def transpose_z(r, pair):
            z_words = z_in[r][:].bitcast(F32)
            if pair == 0:
                zT_ps[r] = []
            if pair < rounds[r][2] // PAIR:
                bank = psum.tile([P, PAIR, 2, P], F32, name="zT_ps")
                for i in range(PAIR):
                    for u in range(2):
                        k = pair * PAIR + i
                        src = zs[r][:, k, u, :] if k < SORT_S else z_words[:, k, u:WORDS:2]
                        nc.tensor.transpose(bank[:, i, u, :], src, ident[:])
                zT_ps[r].append(bank)

        def hidden_leaves_psum(r):
            n = rounds[r][2]
            if H_V and n == ROUND:
                sl = slice(4 - 2 * H_V, 4)
                nc.vector.tensor_copy(out=hT_sb[r][:, sl, :], in_=hT_ps[r][:, sl, :])

        def leave_psum(r):
            leave_h(r)
            leave_z0(r)
            leave_z1(r)

        def squash_a(r):
            squash(r, slice(0, PAIR))

        def squash_b(r):
            if rounds[r][2] > PAIR:
                squash(r, slice(PAIR, ROUND))

        def weigh_early(r):
            n = rounds[r][2]
            gated[r] = work.tile([P, n, CH], F32, name="gated", bufs=SUMLAG + 1 + SB)
            late = [pair_index(r) - p <= VTAIL for p in range(n // PAIR)]
            if r == ROUNDS - 1:
                for p in range(n // PAIR):
                    kids = slice(p * PAIR, p * PAIR + PAIR)
                    weigh(nc.vector if late[p] else nc.gpsimd, r, kids)
                return
            m = sum(1 for x in late if not x) * PAIR
            if m == ROUND and pair_index(r) > WT:
                m -= VM
            if m:
                weigh(nc.gpsimd, r, slice(0, m))

        def leave_z0(r):
            leave_z(r, 0)

        def leave_z1(r):
            if rounds[r][2] > PAIR:
                leave_z(r, 1)

        def leave_h(r):
            n = rounds[r][2]
            hT_sb[r] = work.tile([P, n, P], F32, name="hT_sb", bufs=TRL + 2)
            k = n - 2 * H_V if n == ROUND else n
            if k:
                nc.scalar.copy(out=hT_sb[r][:, 0:k, :], in_=hT_ps[r][:, 0:k, :])

        def leave_z(r, pair):
            n = rounds[r][2]
            if pair == 0:
                grouped[r] = []
            if QW and pair == 0:
                grouped[r].append(work.tile([P, n, P, 4], BF16, name="grouped", bufs=TRL + 2, align_bytes=64))
            if QW:
                half = grouped[r][0][:, pair * PAIR : pair * PAIR + PAIR]
            else:
                values = work.tile([P, PAIR, P, 4], BF16, name="grouped", bufs=2 * TRL, align_bytes=64)
                half = values[:]
                grouped[r].append(values)
            nc.scalar.copy(out=half.bitcast(F32), in_=zT_ps[r][pair][:].rearrange("p i u b -> p i b u"))

        def quantise(r, pairs=(0, 1)):
            if 0 in pairs:
                z_codes[r] = []
                z_scales[r] = []
            if QW:
                n = rounds[r][2]
                codes = work.tile([P, n * P], U32, name="codes", align_bytes=64)
                scales = work.tile([P, n * P], U8, name="scales", align_bytes=64)
                nc.vector.quantize_mx(
                    out=codes[:].bitcast(FP8X4),
                    scales=scales[:],
                    in_=grouped[r][0][:].rearrange("p i b t -> p (i b t)"),
                )
                for pair in range(n // PAIR):
                    cols = slice(pair * PAIR * P, (pair + 1) * PAIR * P)
                    z_codes[r].append(codes[:, cols])
                    z_scales[r].append(scales[:, cols])
                return
            for pair in [p for p in pairs if p < rounds[r][2] // PAIR]:
                codes = work.tile([P, PAIR * P], U32, name="codes", align_bytes=64)
                scales = work.tile([P, PAIR * P], U8, name="scales", align_bytes=64)
                nc.vector.quantize_mx(
                    out=codes[:].bitcast(FP8X4),
                    scales=scales[:],
                    in_=grouped[r][pair][:].rearrange("p i b t -> p (i b t)"),
                )
                z_codes[r].append(codes)
                z_scales[r].append(scales)

        def quantise_first(r):
            quantise(r, (0,))

        def quantise_second(r):
            quantise(r, (1,))

        def multiply_plain(r, child):
            if child >= rounds[r][2]:
                return
            hT = hT_sb[r][:].bitcast(BF16).rearrange("p i (b e) -> p i b e", e=2)
            pair, i = divmod(child, PAIR)
            if child == 0:
                hu_ps[r] = []
            if i == 0:
                hu_ps[r].append(bank_tile([P, PAIR, CH], "hu%d" % pair))
            bank = hu_ps[r][pair]
            for e in range(2):
                nc.tensor.matmul(
                    bank[:, i, :],
                    lhsT=hT[:, child, :, e],
                    rhs=uT[:, e, :],
                    start=(e == 0),
                    stop=(e == 1),
                )

        def multiply_mx(r):
            n = rounds[r][2]
            mx_ps[r] = {}
            for pair in reversed(range(n // PAIR)) if MXREV else range(n // PAIR):
                bank = bank_tile([P, PAIR, CH], "mx%d" % pair)
                for i in range(PAIR):
                    nc.tensor.matmul_mx(
                        out=bank[:, i, :],
                        lhsT=z_codes[r][pair][:, i * P : (i + 1) * P].bitcast(FP8X4),
                        lhsT_scale=z_scales[r][pair][:, i * P : (i + 1) * P],
                        rhs=w_codes[:].bitcast(FP4X4),
                        rhs_scale=w_scales[:],
                        start=True,
                        stop=True,
                    )
                mx_ps[r][pair] = bank

        def add_terms(r):
            n = rounds[r][2]
            gate[r] = work.tile([P, n, CH], F32, name="gate")
            first = gate[r][:, 0:PAIR, :]
            if n == PAIR:
                if QMID >= 0 and "b" in VMID:
                    run(quantise_second, r + 1)
                elif QMID >= 0:
                    run(quantise, r + 1)
                    run(pre_add, r - 2)
                    run(alloc_gated, r - 1)
                    run(weigh_late, r - 1)
                nc.vector.tensor_tensor(out=first, in0=hu_ps[r][0][:], in1=bias, op=ADD)
                nc.vector.tensor_tensor(out=first, in0=mx_ps[r][0][:], in1=first, op=ADD)
                return
            second = gate[r][:, PAIR:ROUND, :]
            h0, h1, m0, m1 = hu_ps[r][0][:], hu_ps[r][1][:], mx_ps[r][0][:], mx_ps[r][1][:]
            seq = {0: [(first, h0, 0), (second, m1, 0), (first, m0, 1), (second, h1, 1)],
                   1: [(first, h0, 0), (first, m0, 1), (second, m1, 0), (second, h1, 1)],
                   2: [(first, m0, 0), (second, m1, 0), (first, h0, 1), (second, h1, 1)],
                   3: [(second, m1, 0), (first, h0, 0), (first, m0, 1), (second, h1, 1)],
                   4: [(second, m1, 0), (first, m0, 0), (first, h0, 1), (second, h1, 1)],
                   5: [(second, m1, 0), (first, m0, 0), (second, h1, 1), (first, h0, 1)]}[ADDORD]
            for k, (o, ps, acc) in enumerate(seq):
                if k == QMID:
                    for word in VMID.split():
                        if word == "q":
                            run(quantise, r + 1)
                        elif word == "b":
                            run(quantise_second, r + 1)
                        elif word == "+":
                            run(pre_add, r - 2)
                        elif word == "m":
                            run(alloc_gated, r - 1)
                            run(weigh_late, r - 1)
                        elif word == "g":
                            run(alloc_gated, r - 1)
                            run(open_window, r - 1)
                nc.vector.tensor_tensor(out=o, in0=ps, in1=o if acc else bias, op=ADD)

        def squash(r, kids):
            nc.scalar.activation(out=gate[r][:, kids, :], in_=gate[r][:, kids, :], func=SIGMOID)

        def weigh(engine, r, kids):
            engine.tensor_tensor(out=gated[r][:, kids, :], in0=gate[r][:, kids, :], in1=zc_in[r][:, kids, CH:SIZE], op=MULT)

        def pair_index(r):
            return sum(x[2] for x in rounds[r:]) // PAIR

        def alloc_gated(r):
            gated[r] = work.tile([P, rounds[r][2], CH], F32, name="gated", bufs=SUMLAG + 1 + SB)

        def squash_only(r):
            if r == ROUNDS - 1:
                for p in range(rounds[r][2] // PAIR):
                    squash(r, slice(p * PAIR, p * PAIR + PAIR))
            else:
                squash(r, slice(0, rounds[r][2]))

        def weigh_g(r):
            n = rounds[r][2]
            late = [pair_index(r) - p <= VTAIL for p in range(n // PAIR)]
            if r == ROUNDS - 1:
                for p in range(n // PAIR):
                    weigh(nc.vector if late[p] else nc.gpsimd, r, slice(p * PAIR, p * PAIR + PAIR))
                return
            m = sum(1 for x in late if not x) * PAIR
            if m == ROUND and pair_index(r) > WT:
                m -= VM
            if m:
                weigh(nc.gpsimd, r, slice(0, m))

        def open_window(r):
            if r < ROUNDS - 1 and pair_index(r) > VTAIL:
                nc.vector.memset(gated[r][:, 0, 0:1], 0.0)

        def squash_and_weigh(r):
            n = rounds[r][2]
            if not GW:
                gated[r] = work.tile([P, n, CH], F32, name="gated", bufs=SUMLAG + 1 + SB)
            late = [pair_index(r) - p <= VTAIL for p in range(n // PAIR)]
            if VOUT and r == ROUNDS - 1:
                late = [True] * (n // PAIR)
            if r == ROUNDS - 1 or PAIRS_SQ:
                for p in range(n // PAIR):
                    kids = slice(p * PAIR, p * PAIR + PAIR)
                    squash(r, kids)
                    if not late[p]:
                        weigh(nc.gpsimd, r, kids)
                    elif r == ROUNDS - 1:
                        weigh(nc.vector, r, kids)
            else:
                squash(r, slice(0, n))
                m = sum(1 for x in late if not x) * PAIR
                if m == ROUND and pair_index(r) > WT:
                    m -= VM
                if m:
                    weigh(nc.gpsimd, r, slice(0, m))
                if GADD and n == ROUND and pair_index(r) > WT:
                    nc.gpsimd.tensor_tensor(out=gated[r][:, 0, :], in0=gated[r][:, 0, :], in1=gated[r][:, 2, :], op=ADD)

        def pre_add(r):
            if VADD and rounds[r][2] == ROUND and pair_index(r) > WT:
                lo = 0
                nc.vector.tensor_tensor(
                    out=gated[r][:, lo : lo + VADD, :],
                    in0=gated[r][:, lo : lo + VADD, :],
                    in1=gated[r][:, ROUND - VADD : ROUND, :],
                    op=ADD,
                )

        def dma_add(r):
            if DADD and rounds[r][2] == ROUND and pair_index(r) > WT:
                nc.gpsimd.dma_start(out=gated[r][:, 0:2, :], in_=gated[r][:, 2:4, :], accum_op=ADD)

        def weigh_late(r):
            n = rounds[r][2]
            if r == ROUNDS - 1:
                return
            if VM and n == ROUND and pair_index(r) > WT:
                weigh(nc.vector, r, slice(ROUND - VM, ROUND))
            for p in range(n // PAIR):
                if pair_index(r) - p <= VTAIL:
                    weigh(nc.vector, r, slice(p * PAIR, p * PAIR + PAIR))

        def add_up(r):
            tile, kid, n, first, last = rounds[r]
            if VOUT:
                if r == ROUNDS - 1:
                    return
                last = last or r == ROUNDS - 2
            if first:
                sumsT_ps[tile] = psum.tile([P, 2, P], F32, name="sumsT_ps", bufs=1)
            kids = list(range(n))
            if (VADD or DADD) and n == ROUND and pair_index(r) > WT:
                kids = kids[: n - (VADD or 2)]
            if GADD and n == ROUND and pair_index(r) > WT:
                kids.remove(2)
            for i in kids:
                for a in range(2):
                    nc.tensor.matmul(
                        sumsT_ps[tile][:, a, :],
                        lhsT=gated[r][:, i, a * P : (a + 1) * P],
                        rhs=ident[:],
                        is_transpose=True,
                        start=(first and i == kids[0] and a == 0),
                        stop=(last and i == kids[-1] and a == 1),
                    )
            if last:
                sumsT_sb[tile] = work.tile([P, 2, P], F32, name="sumsT_sb", bufs=2)
                nc.scalar.copy(out=sumsT_sb[tile][:], in_=sumsT_ps[tile][:])

        def store(r):
            tile, kid, n, first, last = rounds[r]
            if VOUT and r == ROUNDS - 2:
                turned[tile] = bank_tile([P, ROUND, P], "h")
                for a in range(2):
                    nc.tensor.transpose(turned[tile][:, a, :], sumsT_sb[tile][:, a, :], ident[:])
                return
            if not last:
                return
            out_sb = work.tile([P, 2, P], F32, name="out_sb", bufs=2)
            if VOUT and r == ROUNDS - 1:
                flat = out_sb[:].rearrange("p a c -> p (a c)")
                nc.vector.tensor_tensor(out=flat, in0=turned[tile][:, 0:2, :].rearrange("p a c -> p (a c)"), in1=gated[r][:, 0, :], op=ADD)
                for i in range(1, n):
                    nc.vector.tensor_tensor(out=flat, in0=flat, in1=gated[r][:, i, :], op=ADD)
            else:
                sums_ps = bank_tile([P, ROUND, P], "h")
                for a in range(2):
                    nc.tensor.transpose(sums_ps[:, a, :], sumsT_sb[tile][:, a, :], ident[:])
                nc.scalar.copy(out=out_sb[:], in_=sums_ps[:, 0:2, :])
            nc.sync.dma_start(
                out=out[tile * P : (tile + 1) * P, :], in_=out_sb[:].rearrange("p a c -> p (a c)")
            )

        done = set()

        def run(stage, r):
            if 0 <= r < ROUNDS and (stage, r) not in done:
                done.add((stage, r))
                stage(r)

        warm = const.tile([P, 2], F32, name="warm")
        nc.vector.memset(warm[:], 0.0)
        nc.scalar.activation(out=warm[:, 1:2], in_=warm[:, 0:1], func=SIGMOID)
        ident = const.tile([P, P], F32, name="ident")
        make_identity(nc, ident[:])
        w_scales = const.tile([P, CH], U8, name="w_scales", align_bytes=64)
        nc.vector.memset(w_scales[:].bitcast(I32), 0)

        u_rows = const.tile([P, 2, CH], BF16, name="u_rows")
        b_pad = const.tile([P, CH], BF16, name="b_pad")
        nc.vector.memset(b_pad[:], 0.0)
        ones = const.tile([P, P], BF16, name="ones")
        nc.vector.memset(ones[:], 1.0)
        bias_rows = const.tile([P, CH], BF16, name="bias_rows")
        w_codes = const.tile([P, 2 * CH], U8, name="w_codes", align_bytes=64)
        ubq = nc.scalar if BQ == "scalar" else nc.sync
        if LOADORD == "u":
            ubq.dma_start(out=u_rows[:], in_=U_f.rearrange("(a p) k -> p a k", p=P))
            load(0)
        else:
            load(0)
            ubq.dma_start(out=u_rows[:], in_=U_f.rearrange("(a p) k -> p a k", p=P))
        nc.sync.dma_start(out=w_codes[:].bitcast(I32), in_=W_f_words[0].bitcast(I32))
        for quadrant in range(4):
            nc.sync.dma_start(
                out=w_scales[32 * quadrant : 32 * quadrant + 4, :].bitcast(I32),
                in_=W_f_scales[0, 4 * quadrant : 4 * quadrant + 4, :].bitcast(I32),
            )
        load(1)
        nc.sync.dma_start(out=b_pad[0:1, :], in_=b_f.unsqueeze(0))
        load(2)
        load(3)

        u_ps = bank_tile([P, ROUND, P], "h")
        for a in range(2):
            nc.tensor.transpose(u_ps[:, a, :], u_rows[:].bitcast(F32)[:, a, :], ident[:])
        uT_words = const.tile([P, 2, P], F32, name="uT_words")
        nc.vector.tensor_copy(out=uT_words[:], in_=u_ps[:, 0:2, :])
        uT = const.tile([P, 2, CH], BF16, name="uT")
        nc.vector.tensor_copy(
            out=uT[:].rearrange("p e (a c) -> p e a c", a=2),
            in_=uT_words[:].bitcast(BF16).rearrange("p a (c e) -> p e a c", e=2),
        )
        bias = bias_rows[:].unsqueeze(1).to_broadcast([P, PAIR, CH])

        def spread_bias():
            bank = bank_tile([P, CH], "mx1")
            nc.tensor.matmul(bank[:], lhsT=ones[:], rhs=b_pad[:], start=True, stop=True)
            nc.vector.tensor_copy(out=bias_rows[:], in_=bank[:])

        for step in range(-TRL - 1, ROUNDS + SUMLAG + 4):
            if step > -TRL - 1:
                run(load, step + TRL + 4)
            if QMID >= 0 and step == -1 and "b" not in VMID:
                run(quantise, 0)
            for word in VPRE.split():
                run({"q": quantise, "a": quantise_first, "+": pre_add, "m": weigh_late}[word], step + {"q": 1, "a": 1, "+": -2, "m": -1}[word])
            if GW == 1:
                run(alloc_gated, step - 1)
                run(open_window, step - 1)
            if GW == 2:
                run(squash_only, step - 1)
            elif not SO:
                run(squash_and_weigh, step - 1)
            for word in PE.split():
                if word[0] == "p":
                    if 0 <= step < ROUNDS:
                        multiply_plain(step, int(word[1]))
                elif word == "m":
                    run(multiply_mx, step)
                    if step == 0:
                        spread_bias()
                elif word == "T":
                    run(store, step - SUMLAG - SB)
                elif word == "S":
                    if SB == 1:
                        run(add_up, step - SUMLAG)
                    elif step % 2 == 0 or step >= ROUNDS:
                        run(add_up, step - SUMLAG - 1)
                        run(add_up, step - SUMLAG)
                elif word == "h":
                    run(transpose_h, step + TRL)
                elif word[0] == "z":
                    if 0 <= step + TRL < ROUNDS:
                        transpose_z(step + TRL, int(word[1]))
            if SQD == 0:
                run(add_terms, step)
            if SO:
                for word in SO.split():
                    if word in ("a", "b"):
                        run(squash_a if word == "a" else squash_b, step - SQD)
                    elif word == "h":
                        run(leave_h, step + TRL)
                    else:
                        run(leave_z0 if word == "0" else leave_z1, step + TRL)
                run(weigh_early, step - SQD)
            else:
                run(leave_psum, step + TRL)
            if "T" not in PE:
                run(store, step - SUMLAG - SB)
            if SQD:
                run(add_terms, step)
            if GW == 2:
                run(alloc_gated, step - 1)
                if step >= ROUNDS:
                    run(weigh_late, step - 1)
                run(weigh_g, step - 1)
                if step >= ROUNDS:
                    run(pre_add, step - 2)
            run(dma_add, step - 2)
            if "b" in VMID and step < 0:
                run(quantise_second, step + 1)
            for word in VPOST.split():
                run({"q": quantise, "a": quantise_first, "+": pre_add, "m": weigh_late}[word], step + {"q": 1, "a": 1, "+": -2, "m": -1}[word])
            run(hidden_leaves_psum, step + TRL)
            rotate()
            run(sort, step + TRL + 1)
